import numpy as np
import ml_dtypes


def mxq(x, axis, fmt="e4m3"):
    dtype, down = {"e4m3": (ml_dtypes.float8_e4m3fn, 7), "e5m2": (ml_dtypes.float8_e5m2, 14)}[fmt]
    v = np.moveaxis(np.asarray(x, np.float32).astype(ml_dtypes.bfloat16).astype(np.float64), axis, -1)
    blocks = v.reshape(v.shape[:-1] + (-1, 32))
    amax = np.abs(blocks).max(-1, keepdims=True)
    byte = np.maximum(np.where(amax > 0, np.frexp(amax)[1] - 1 + 127, 0) - down, 1)
    scale = np.exp2(byte - 127.0)
    codes = (blocks / scale).astype(np.float32).astype(dtype).astype(np.float64)
    return np.moveaxis((codes * scale).reshape(v.shape), -1, axis)


WIDE = False


def mx_kscale(k):
    if not WIDE:
        return np.ones(k)
    levels = np.array([10, -10, 5, -5, 0])
    a = np.random.permutation(np.resize(levels, k // 512 * 4)).reshape(k // 512, 4)
    idx = np.arange(k)
    return np.exp2(a[idx // 512, idx % 128 // 32])


BF16 = ml_dtypes.bfloat16


def bf(x):
    return np.asarray(x, np.float32).astype(BF16)


def f64(x):
    return np.asarray(x).astype(np.float64)


N, D_IN, H0, H1, K = 512, 16384, 512, 256, 20
V = 1.0


def silu(v):
    return v / (1.0 + np.exp(-v))


def setup_inputs():
    s = mx_kscale(D_IN)
    w1 = np.random.standard_normal((D_IN, H0)) / np.sqrt(D_IN)
    b1 = np.random.standard_normal(H0) * 0.2
    w2 = np.random.standard_normal((H0, H1)) * 4.0 / np.sqrt(H0 * H1)
    b2 = np.random.standard_normal(H1) * 0.1
    cent = np.random.standard_normal((K, D_IN)) * 0.9
    x = cent[np.random.randint(0, K, N)] + np.random.standard_normal((N, D_IN)) * 0.44
    hc = silu(np.stack([(c[:, None] * w1).sum(0) for c in cent]) + b1)
    clusters = (hc[:, :, None] * w2[None]).sum(1) + b2 + np.random.standard_normal((K, H1)) * 0.5 / np.sqrt(H1)
    return {"x": bf(x * s), "W1": bf(w1 / s[:, None]), "b1": bf(b1), "W2": bf(w2), "b2": bf(b2), "clusters": bf(clusters)}


def reference(x, W1, b1, W2, b2, clusters):
    h = silu((mxq(f64(x), 1, "e4m3") @ mxq(f64(W1), 0, "e4m3")) + f64(b1))
    z = (mxq(h, 1, "e4m3") @ mxq(f64(W2), 0, "e4m3")) + f64(b2)
    d2 = np.stack([((z - c) ** 2).sum(1) for c in f64(clusters)], axis=1)
    q = 1.0 / (1.0 + d2 / V)
    q = q ** ((V + 1.0) / 2.0)
    q = q / q.sum(1, keepdims=True)
    return z, q

@@ -1,0 +1,363 @@
+from contextlib import ExitStack
+
+import concourse.mybir as mybir
+from concourse.masks import make_identity
+
+F32 = mybir.dt.float32
+BF16 = mybir.dt.bfloat16
+U32 = mybir.dt.uint32
+U8 = mybir.dt.uint8
+FP8X4 = mybir.dt.float8_e4m3fn_x4
+ACT = mybir.ActivationFunctionType
+ALU = mybir.AluOpType
+
+P = 128
+PACK = 4
+K_PASS = P * PACK
+N_ROWS, D_IN, H0, H1, N_CLUSTERS = 512, 16384, 512, 256, 20
+ROW_TILES = N_ROWS // P
+H0_TILES = H0 // P
+H1_TILES = H1 // P
+PASSES = D_IN // K_PASS
+WORDS = K_PASS // 2
+
+FLOPS = 2 * N_ROWS * D_IN * H0 + 2 * N_ROWS * H0 * H1 + 3 * N_ROWS * H1 * N_CLUSTERS
+
+LONG_CHUNK = 4
+TAPER = [1, 1, 2]
+CHUNKS = TAPER + [LONG_CHUNK] * ((PASSES - 2 * sum(TAPER)) // LONG_CHUNK) + TAPER[::-1]
+assert sum(CHUNKS) == PASSES
+RAW_BUFS = 4
+
+LAG = 2
+
+W_COLS_VECTOR = 320
+
+
+def tile_lintrans_pa_k_kernel(tc, x, W1, b1, W2, b2, clusters, out_0, out_1):
+    nc = tc.nc
+    with ExitStack() as ctx:
+        const = ctx.enter_context(tc.tile_pool(name="const", bufs=1))
+        x_pool = ctx.enter_context(tc.tile_pool(name="x_pool", bufs=RAW_BUFS))
+        w_pool = ctx.enter_context(tc.tile_pool(name="w_pool", bufs=RAW_BUFS))
+        grouped_pool = ctx.enter_context(tc.tile_pool(name="grouped_pool", bufs=4))
+        code_pool = ctx.enter_context(tc.tile_pool(name="code_pool", bufs=4))
+        acc_pool = ctx.enter_context(tc.psum_pool(name="acc_pool", bufs=1))
+        work_pool = ctx.enter_context(tc.psum_pool(name="work_pool", bufs=4))
+        ctx.enter_context(tc.manual_schedule())
+
+        x_rows = x.rearrange("(p i) k -> p i k", i=ROW_TILES)
+        w_rows = W1.rearrange("(s p e) n -> p s (e n)", p=P, e=2)
+        chunk_first = [sum(CHUNKS[:c]) for c in range(len(CHUNKS))]
+        chunk_of_pass = [c for c in range(len(CHUNKS)) for repeat in range(CHUNKS[c])]
+        raw = {}
+
+        def load_chunk(c):
+            first, count = chunk_first[c], CHUNKS[c]
+            w_raw = w_pool.tile([P, 2 * LONG_CHUNK, 2 * H0], BF16)
+            nc.sync.dma_start(
+                out=w_raw[:, 0 : 2 * count, :], in_=w_rows[:, 2 * first : 2 * (first + count), :]
+            )
+            x_raw = x_pool.tile([P, ROW_TILES, LONG_CHUNK * K_PASS], BF16)
+            nc.sync.dma_start(
+                out=x_raw[:, :, 0 : count * K_PASS],
+                in_=x_rows[:, :, first * K_PASS : (first + count) * K_PASS],
+            )
+            raw[c] = (x_raw, w_raw)
+
+        for c in range(RAW_BUFS):
+            load_chunk(c)
+
+        ident = const.tile([P, P], F32)
+        make_identity(nc, ident[:])
+        ones = const.tile([P, P], F32)
+        nc.gpsimd.memset(ones[:], 1.0)
+        B1_ROW, B2_ROW, CLUSTER_ROW, CLUSTER_PITCH = 0, 4, 32, 32
+        small_rows = const.tile([P, P], BF16)
+        nc.gpsimd.memset(small_rows[:], 0.0)
+        nc.scalar.dma_start(
+            out=small_rows[B1_ROW : B1_ROW + H0_TILES, :], in_=b1.rearrange("(m p) -> m p", p=P)
+        )
+        nc.scalar.dma_start(
+            out=small_rows[B2_ROW : B2_ROW + H1_TILES, :], in_=b2.rearrange("(m p) -> m p", p=P)
+        )
+        for half in range(H1_TILES):
+            row = CLUSTER_ROW + CLUSTER_PITCH * half
+            nc.scalar.dma_start(
+                out=small_rows[row : row + N_CLUSTERS, :], in_=clusters[:, P * half : P * (half + 1)]
+            )
+        w2_raw = const.tile([P, PACK, H1], BF16)
+        nc.scalar.dma_start(out=w2_raw[:], in_=W2.rearrange("(t p) j -> p t j", p=P))
+        table_warm = const.tile([P, 1], F32)
+        nc.scalar.activation(out=table_warm[:], in_=ones[:, 0:1], func=ACT.Silu)
+
+        small_cols = const.tile([P, P], F32)
+        b1_col = small_cols[:, B1_ROW : B1_ROW + H0_TILES]
+        b2_col = small_cols[:, B2_ROW : B2_ROW + H1_TILES]
+        clusters_t = small_cols[
+            :, CLUSTER_ROW : CLUSTER_ROW + CLUSTER_PITCH * H1_TILES
+        ].rearrange("p (m k) -> p m k", m=H1_TILES)[:, :, 0:N_CLUSTERS]
+        minus_2c = const.tile([P, H1_TILES, N_CLUSTERS], F32)
+        c_squared = const.tile([P, H1_TILES, N_CLUSTERS], F32)
+        b2_spread = const.tile([P, H1], F32)
+        c_norm_plus_1 = const.tile([P, N_CLUSTERS], F32)
+        w2_codes = const.tile([P, H1], U32, align_bytes=64)
+        w2_scales = const.tile([P, H1], U8, align_bytes=64)
+
+        def turn_small_rows_into_columns():
+            small_rows_f32 = const.tile([P, P], F32)
+            nc.vector.tensor_copy(out=small_rows_f32[:], in_=small_rows[:])
+            turned = acc_pool.tile([P, P], F32, tag="acc0")
+            nc.tensor.transpose(turned[:], small_rows_f32[:], ident[:])
+            nc.vector.tensor_copy(out=small_cols[:], in_=turned[:])
+            nc.vector.tensor_scalar(
+                out=minus_2c[:], in0=clusters_t, scalar1=-2.0, scalar2=None, op0=ALU.mult
+            )
+            nc.vector.tensor_tensor(out=c_squared[:], in0=clusters_t, in1=clusters_t, op=ALU.mult)
+
+        def spread_b2_and_centroid_norms():
+            spread = acc_pool.tile([P, 2 * H1], F32, tag="acc0")
+            for half in range(H1_TILES):
+                nc.tensor.matmul(
+                    out=spread[:, P * half : P * (half + 1)],
+                    lhsT=b2_col[:, half : half + 1].to_broadcast([P, P]),
+                    rhs=ident[:],
+                    start=True,
+                    stop=True,
+                )
+            for half in range(H1_TILES):
+                nc.tensor.matmul(
+                    out=spread[:, H1 : H1 + N_CLUSTERS],
+                    lhsT=ones[:],
+                    rhs=c_squared[:, half, :],
+                    start=(half == 0),
+                    stop=(half == H1_TILES - 1),
+                )
+            nc.vector.tensor_copy(out=b2_spread[:], in_=spread[:, 0:H1])
+            nc.vector.tensor_scalar(
+                out=c_norm_plus_1[:],
+                in0=spread[:, H1 : H1 + N_CLUSTERS],
+                scalar1=1.0,
+                scalar2=None,
+                op0=ALU.add,
+            )
+            w2_grouped = const.tile([P, H1, PACK], BF16, align_bytes=64)
+            nc.vector.tensor_copy(
+                out=w2_grouped[:].rearrange("p (c i) t -> p c t i", i=4),
+                in_=w2_raw[:].rearrange("p t (c i) -> p c t i", i=4),
+            )
+            nc.vector.quantize_mx(
+                out=w2_codes[:].bitcast(FP8X4),
+                scales=w2_scales[:],
+                in_=w2_grouped[:].rearrange("p j t -> p (j t)"),
+            )
+
+        small_work = [turn_small_rows_into_columns, spread_b2_and_centroid_norms]
+        assert len(small_work) == LAG
+
+        X_PART, W_PART = 0, N_ROWS
+        grouped = {}
+        transposed = {}
+        codes = {}
+        acc = []
+
+        def regroup_w(g):
+            c = chunk_of_pass[g]
+            local = g - chunk_first[c]
+            grouped[g] = grouped_pool.tile(
+                [P, (N_ROWS + H0) * PACK], BF16, align_bytes=64, name="grouped"
+            )
+            rows = raw[c][1][:, 2 * local : 2 * local + 2, :].rearrange(
+                "p u (e n) -> p (u e) n", e=2
+            )
+            words = grouped[g][:, W_PART * PACK :].rearrange("p (n t) -> p n t", t=PACK)
+            vector_cols = slice(0, W_COLS_VECTOR)
+            scalar_cols = slice(W_COLS_VECTOR, H0)
+            nc.vector.tensor_copy(
+                out=words[:, vector_cols, :].rearrange("p (c i) t -> p c t i", i=4),
+                in_=rows[:, :, vector_cols].rearrange("p t (c i) -> p c t i", i=4),
+            )
+            nc.scalar.copy(
+                out=words[:, scalar_cols, :].rearrange("p (c i) t -> p c t i", i=4),
+                in_=rows[:, :, scalar_cols].rearrange("p t (c i) -> p c t i", i=4),
+            )
+
+        def transpose_x(g):
+            c = chunk_of_pass[g]
+            local = g - chunk_first[c]
+            x_words = raw[c][0][:].bitcast(F32)
+            transposed[g] = []
+            for bank in range(2):
+                turned = work_pool.tile([P, 2, 2 * P], F32, tag="work")
+                for u in range(2):
+                    for j in range(2):
+                        first_word = WORDS * local + P * u
+                        nc.tensor.transpose(
+                            turned[:, u, P * j : P * (j + 1)],
+                            x_words[:, 2 * bank + j, first_word : first_word + P],
+                            ident[:],
+                        )
+                transposed[g].append(turned)
+
+        def copy_x(g):
+            pairs = grouped[g][:].bitcast(F32)[:, 0 : N_ROWS * 2].rearrange(
+                "p (c u) -> p c u", u=2
+            )
+            for bank in range(2):
+                nc.scalar.copy(
+                    out=pairs[:, 2 * P * bank : 2 * P * (bank + 1), :],
+                    in_=transposed[g][bank][:].rearrange("p u c -> p c u"),
+                )
+
+        def quantise(g):
+            words = code_pool.tile([P, N_ROWS + H0], U32, align_bytes=64, name="words")
+            scales = code_pool.tile([P, N_ROWS + H0], U8, align_bytes=64, name="scales")
+            nc.vector.quantize_mx(out=words[:].bitcast(FP8X4), scales=scales[:], in_=grouped[g][:])
+            codes[g] = (words, scales)
+
+        def multiply(g):
+            words, scales = codes[g]
+            for m in range(H0_TILES):
+                if g == 0:
+                    acc.append(acc_pool.tile([P, N_ROWS], F32, name="acc%d" % m))
+                w_cols = slice(W_PART + P * m, W_PART + P * (m + 1))
+                x_cols = slice(X_PART, X_PART + N_ROWS)
+                nc.tensor.matmul_mx(
+                    out=acc[m][:],
+                    lhsT=words[:, w_cols].bitcast(FP8X4),
+                    lhsT_scale=scales[:, w_cols],
+                    rhs=words[:, x_cols].bitcast(FP8X4),
+                    rhs_scale=scales[:, x_cols],
+                    start=(g == 0),
+                    stop=(g == PASSES - 1),
+                )
+
+        regroup_w(0)
+        for step in range(PASSES + LAG):
+            if step < PASSES:
+                transpose_x(step)
+                copy_x(step)
+                c = chunk_of_pass[step]
+                is_last_of_chunk = step + 1 == chunk_first[c] + CHUNKS[c]
+                if is_last_of_chunk and c + RAW_BUFS < len(CHUNKS):
+                    load_chunk(c + RAW_BUFS)
+            if step < LAG:
+                small_work[step]()
+            if step + 1 < PASSES:
+                regroup_w(step + 1)
+            if step < PASSES:
+                quantise(step)
+            if step >= LAG:
+                multiply(step - LAG)
+
+        h_planes = const.tile([P, PACK, N_ROWS], BF16)
+        for m in range(H0_TILES):
+            nc.scalar.activation(
+                out=h_planes[:, m, :], in_=acc[m][:], func=ACT.Silu, bias=b1_col[:, m : m + 1]
+            )
+        h_grouped = const.tile([P, N_ROWS, PACK], BF16, align_bytes=64)
+        nc.vector.tensor_copy(
+            out=h_grouped[:].rearrange("p (c i) t -> p c t i", i=4),
+            in_=h_planes[:].rearrange("p t (c i) -> p c t i", i=4),
+        )
+        h_codes = const.tile([P, N_ROWS], U32, align_bytes=64)
+        h_scales = const.tile([P, N_ROWS], U8, align_bytes=64)
+        nc.vector.quantize_mx(
+            out=h_codes[:].bitcast(FP8X4),
+            scales=h_scales[:],
+            in_=h_grouped[:].rearrange("p c t -> p (c t)"),
+        )
+
+        zt_psum = []
+        for half in range(H1_TILES):
+            j_cols = slice(P * half, P * (half + 1))
+            zt_bank = work_pool.tile([P, N_ROWS], F32, tag="work")
+            nc.tensor.matmul_mx(
+                out=zt_bank[:],
+                lhsT=w2_codes[:, j_cols].bitcast(FP8X4),
+                lhsT_scale=w2_scales[:, j_cols],
+                rhs=h_codes[:].bitcast(FP8X4),
+                rhs_scale=h_scales[:],
+                start=True,
+                stop=True,
+            )
+            zt_psum.append(zt_bank)
+        z_psum = []
+        for bank in range(2):
+            z_bank = work_pool.tile([P, 2, H1], F32, tag="work")
+            for j in range(2):
+                row_cols = slice(P * (2 * bank + j), P * (2 * bank + j + 1))
+                nc.tensor.matmul_mx(
+                    out=z_bank[:, j, :],
+                    lhsT=h_codes[:, row_cols].bitcast(FP8X4),
+                    lhsT_scale=h_scales[:, row_cols],
+                    rhs=w2_codes[:].bitcast(FP8X4),
+                    rhs_scale=w2_scales[:],
+                    start=True,
+                    stop=True,
+                )
+            z_psum.append(z_bank)
+
+        zt_0 = const.tile([P, N_ROWS], F32)
+        nc.scalar.activation(out=zt_0[:], in_=zt_psum[0][:], func=ACT.Identity, bias=b2_col[:, 0:1])
+        zt_1 = const.tile([P, N_ROWS], F32)
+        nc.vector.tensor_scalar(
+            out=zt_1[:], in0=zt_psum[1][:], scalar1=b2_col[:, 1:2], scalar2=None, op0=ALU.add
+        )
+        zt = [zt_0, zt_1]
+
+        z_sb = const.tile([P, ROW_TILES, H1], F32)
+        for bank in range(2):
+            nc.vector.tensor_tensor(
+                out=z_sb[:, 2 * bank : 2 * bank + 2, :],
+                in0=z_psum[bank][:],
+                in1=b2_spread[:].unsqueeze(1).to_broadcast([P, 2, H1]),
+                op=ALU.add,
+            )
+        nc.sync.dma_start(out=out_0.rearrange("(p i) j -> p i j", i=ROW_TILES), in_=z_sb[:])
+
+        CLUSTER_SLOT = 32
+        cross = work_pool.tile([P, ROW_TILES, CLUSTER_SLOT], F32, tag="work")
+        for i in range(ROW_TILES):
+            for half in range(H1_TILES):
+                nc.tensor.matmul(
+                    out=cross[:, i, 0:N_CLUSTERS],
+                    lhsT=zt[half][:, P * i : P * (i + 1)],
+                    rhs=minus_2c[:, half, :],
+                    start=(half == 0),
+                    stop=(half == H1_TILES - 1),
+                )
+        z_norm = const.tile([P, ROW_TILES], F32)
+        z_squared = const.tile([P, H1], F32)
+        for i in range(ROW_TILES):
+            nc.scalar.activation(
+                out=z_squared[:], in_=z_sb[:, i, :], func=ACT.Square, accum_out=z_norm[:, i : i + 1]
+            )
+        q_shape = [P, ROW_TILES, N_CLUSTERS]
+        norms = const.tile(q_shape, F32)
+        nc.vector.tensor_tensor(
+            out=norms[:],
+            in0=c_norm_plus_1[:].unsqueeze(1).to_broadcast(q_shape),
+            in1=z_norm[:].unsqueeze(2).to_broadcast(q_shape),
+            op=ALU.add,
+        )
+        one_plus_d2 = const.tile(q_shape, F32)
+        nc.vector.tensor_tensor(
+            out=one_plus_d2[:], in0=cross[:, :, 0:N_CLUSTERS], in1=norms[:], op=ALU.add
+        )
+        t_kernel = const.tile(q_shape, F32)
+        nc.vector.reciprocal(out=t_kernel[:], in_=one_plus_d2[:])
+        t_sum = const.tile([P, ROW_TILES], F32)
+        nc.vector.tensor_reduce(
+            out=t_sum[:], in_=t_kernel[:], axis=mybir.AxisListType.X, op=ALU.add
+        )
+        t_sum_inverse = const.tile([P, ROW_TILES], F32)
+        nc.vector.reciprocal(out=t_sum_inverse[:], in_=t_sum[:])
+        q_sb = const.tile(q_shape, F32)
+        nc.vector.tensor_tensor(
+            out=q_sb[:],
+            in0=t_kernel[:],
+            in1=t_sum_inverse[:].unsqueeze(2).to_broadcast(q_shape),
+            op=ALU.mult,
+        )
+        nc.sync.dma_start(out=out_1.rearrange("(p i) k -> p i k", i=ROW_TILES), in_=q_sb[:])

@@ -28,6 +28,7 @@ TAPER = [1, 1, 2]
 CHUNKS = TAPER + [LONG_CHUNK] * ((PASSES - 2 * sum(TAPER)) // LONG_CHUNK) + TAPER[::-1]
 assert sum(CHUNKS) == PASSES
 RAW_BUFS = 4
+RUNS_PER_DMA = 4
 
 LAG = 2
 
@@ -55,14 +56,18 @@ def tile_lintrans_pa_k_kernel(tc, x, W1, b1, W2, b2, clusters, out_0, out_1):
         def load_chunk(c):
             first, count = chunk_first[c], CHUNKS[c]
             w_raw = w_pool.tile([P, 2 * LONG_CHUNK, 2 * H0], BF16)
-            nc.sync.dma_start(
-                out=w_raw[:, 0 : 2 * count, :], in_=w_rows[:, 2 * first : 2 * (first + count), :]
-            )
             x_raw = x_pool.tile([P, ROW_TILES, LONG_CHUNK * K_PASS], BF16)
-            nc.sync.dma_start(
-                out=x_raw[:, :, 0 : count * K_PASS],
-                in_=x_rows[:, :, first * K_PASS : (first + count) * K_PASS],
-            )
+            for s in range(0, 2 * count, RUNS_PER_DMA):
+                runs = min(RUNS_PER_DMA, 2 * count - s)
+                nc.sync.dma_start(
+                    out=w_raw[:, s : s + runs, :],
+                    in_=w_rows[:, 2 * first + s : 2 * first + s + runs, :],
+                )
+                if s == 0:
+                    nc.sync.dma_start(
+                        out=x_raw[:, :, 0 : count * K_PASS],
+                        in_=x_rows[:, :, first * K_PASS : (first + count) * K_PASS],
+                    )
             raw[c] = (x_raw, w_raw)
 
         for c in range(RAW_BUFS):
@@ -75,19 +80,19 @@ def tile_lintrans_pa_k_kernel(tc, x, W1, b1, W2, b2, clusters, out_0, out_1):
         B1_ROW, B2_ROW, CLUSTER_ROW, CLUSTER_PITCH = 0, 4, 32, 32
         small_rows = const.tile([P, P], BF16)
         nc.gpsimd.memset(small_rows[:], 0.0)
-        nc.scalar.dma_start(
+        nc.sync.dma_start(
             out=small_rows[B1_ROW : B1_ROW + H0_TILES, :], in_=b1.rearrange("(m p) -> m p", p=P)
         )
-        nc.scalar.dma_start(
+        nc.sync.dma_start(
             out=small_rows[B2_ROW : B2_ROW + H1_TILES, :], in_=b2.rearrange("(m p) -> m p", p=P)
         )
         for half in range(H1_TILES):
             row = CLUSTER_ROW + CLUSTER_PITCH * half
-            nc.scalar.dma_start(
+            nc.sync.dma_start(
                 out=small_rows[row : row + N_CLUSTERS, :], in_=clusters[:, P * half : P * (half + 1)]
             )
         w2_raw = const.tile([P, PACK, H1], BF16)
-        nc.scalar.dma_start(out=w2_raw[:], in_=W2.rearrange("(t p) j -> p t j", p=P))
+        nc.sync.dma_start(out=w2_raw[:], in_=W2.rearrange("(t p) j -> p t j", p=P))
         table_warm = const.tile([P, 1], F32)
         nc.scalar.activation(out=table_warm[:], in_=ones[:, 0:1], func=ACT.Silu)
 
@@ -107,7 +112,7 @@ def tile_lintrans_pa_k_kernel(tc, x, W1, b1, W2, b2, clusters, out_0, out_1):
         def turn_small_rows_into_columns():
             small_rows_f32 = const.tile([P, P], F32)
             nc.vector.tensor_copy(out=small_rows_f32[:], in_=small_rows[:])
-            turned = acc_pool.tile([P, P], F32, tag="acc0")
+            turned = work_pool.tile([P, P], F32, tag="work")
             nc.tensor.transpose(turned[:], small_rows_f32[:], ident[:])
             nc.vector.tensor_copy(out=small_cols[:], in_=turned[:])
             nc.vector.tensor_scalar(
@@ -116,7 +121,7 @@ def tile_lintrans_pa_k_kernel(tc, x, W1, b1, W2, b2, clusters, out_0, out_1):
             nc.vector.tensor_tensor(out=c_squared[:], in0=clusters_t, in1=clusters_t, op=ALU.mult)
 
         def spread_b2_and_centroid_norms():
-            spread = acc_pool.tile([P, 2 * H1], F32, tag="acc0")
+            spread = work_pool.tile([P, 2 * H1], F32, tag="work")
             for half in range(H1_TILES):
                 nc.tensor.matmul(
                     out=spread[:, P * half : P * (half + 1)],
@@ -152,8 +157,10 @@ def tile_lintrans_pa_k_kernel(tc, x, W1, b1, W2, b2, clusters, out_0, out_1):
                 in_=w2_grouped[:].rearrange("p j t -> p (j t)"),
             )
 
-        small_work = [turn_small_rows_into_columns, spread_b2_and_centroid_norms]
-        assert len(small_work) == LAG
+        small_work = {
+            PASSES // 2: turn_small_rows_into_columns,
+            PASSES // 2 + 1: spread_b2_and_centroid_norms,
+        }
 
         X_PART, W_PART = 0, N_ROWS
         grouped = {}
@@ -241,7 +248,7 @@ def tile_lintrans_pa_k_kernel(tc, x, W1, b1, W2, b2, clusters, out_0, out_1):
                 is_last_of_chunk = step + 1 == chunk_first[c] + CHUNKS[c]
                 if is_last_of_chunk and c + RAW_BUFS < len(CHUNKS):
                     load_chunk(c + RAW_BUFS)
-            if step < LAG:
+            if step in small_work:
                 small_work[step]()
             if step + 1 < PASSES:
                 regroup_w(step + 1)
@@ -250,45 +257,60 @@ def tile_lintrans_pa_k_kernel(tc, x, W1, b1, W2, b2, clusters, out_0, out_1):
             if step >= LAG:
                 multiply(step - LAG)
 
+        HALVES = 2
+        HALF = N_ROWS // HALVES
+        TILES_PER_HALF = ROW_TILES // HALVES
+        half_cols = [slice(HALF * a, HALF * (a + 1)) for a in range(HALVES)]
+        half_tiles = [slice(TILES_PER_HALF * a, TILES_PER_HALF * (a + 1)) for a in range(HALVES)]
+
         h_planes = const.tile([P, PACK, N_ROWS], BF16)
-        for m in range(H0_TILES):
-            nc.scalar.activation(
-                out=h_planes[:, m, :], in_=acc[m][:], func=ACT.Silu, bias=b1_col[:, m : m + 1]
-            )
+        for a in range(HALVES):
+            for m in range(H0_TILES):
+                nc.scalar.activation(
+                    out=h_planes[:, m, half_cols[a]],
+                    in_=acc[m][:, half_cols[a]],
+                    func=ACT.Silu,
+                    bias=b1_col[:, m : m + 1],
+                )
         h_grouped = const.tile([P, N_ROWS, PACK], BF16, align_bytes=64)
-        nc.vector.tensor_copy(
-            out=h_grouped[:].rearrange("p (c i) t -> p c t i", i=4),
-            in_=h_planes[:].rearrange("p t (c i) -> p c t i", i=4),
-        )
         h_codes = const.tile([P, N_ROWS], U32, align_bytes=64)
         h_scales = const.tile([P, N_ROWS], U8, align_bytes=64)
-        nc.vector.quantize_mx(
-            out=h_codes[:].bitcast(FP8X4),
-            scales=h_scales[:],
-            in_=h_grouped[:].rearrange("p c t -> p (c t)"),
-        )
-
-        zt_psum = []
-        for half in range(H1_TILES):
-            j_cols = slice(P * half, P * (half + 1))
-            zt_bank = work_pool.tile([P, N_ROWS], F32, tag="work")
-            nc.tensor.matmul_mx(
-                out=zt_bank[:],
-                lhsT=w2_codes[:, j_cols].bitcast(FP8X4),
-                lhsT_scale=w2_scales[:, j_cols],
-                rhs=h_codes[:].bitcast(FP8X4),
-                rhs_scale=h_scales[:],
-                start=True,
-                stop=True,
+        for a in range(HALVES):
+            nc.vector.tensor_copy(
+                out=h_grouped[:, half_cols[a], :].rearrange("p (c i) t -> p c t i", i=4),
+                in_=h_planes[:, :, half_cols[a]].rearrange("p t (c i) -> p c t i", i=4),
             )
-            zt_psum.append(zt_bank)
-        z_psum = []
-        for bank in range(2):
-            z_bank = work_pool.tile([P, 2, H1], F32, tag="work")
-            for j in range(2):
-                row_cols = slice(P * (2 * bank + j), P * (2 * bank + j + 1))
+            nc.vector.quantize_mx(
+                out=h_codes[:, half_cols[a]].bitcast(FP8X4),
+                scales=h_scales[:, half_cols[a]],
+                in_=h_grouped[:, half_cols[a], :].rearrange("p c t -> p (c t)"),
+            )
+
+        zt_psum = [
+            work_pool.tile([P, N_ROWS], F32, tag="work", name="zt_psum%d" % m)
+            for m in range(H1_TILES)
+        ]
+        z_psum = [
+            work_pool.tile([P, TILES_PER_HALF, H1], F32, tag="work", name="z_psum%d" % a)
+            for a in range(HALVES)
+        ]
+        for a in range(HALVES):
+            for m in range(H1_TILES):
+                j_cols = slice(P * m, P * (m + 1))
                 nc.tensor.matmul_mx(
-                    out=z_bank[:, j, :],
+                    out=zt_psum[m][:, half_cols[a]],
+                    lhsT=w2_codes[:, j_cols].bitcast(FP8X4),
+                    lhsT_scale=w2_scales[:, j_cols],
+                    rhs=h_codes[:, half_cols[a]].bitcast(FP8X4),
+                    rhs_scale=h_scales[:, half_cols[a]],
+                    start=True,
+                    stop=True,
+                )
+            for j in range(TILES_PER_HALF):
+                i = TILES_PER_HALF * a + j
+                row_cols = slice(P * i, P * (i + 1))
+                nc.tensor.matmul_mx(
+                    out=z_psum[a][:, j, :],
                     lhsT=h_codes[:, row_cols].bitcast(FP8X4),
                     lhsT_scale=h_scales[:, row_cols],
                     rhs=w2_codes[:].bitcast(FP8X4),
@@ -296,36 +318,42 @@ def tile_lintrans_pa_k_kernel(tc, x, W1, b1, W2, b2, clusters, out_0, out_1):
                     start=True,
                     stop=True,
                 )
-            z_psum.append(z_bank)
 
-        zt_0 = const.tile([P, N_ROWS], F32)
-        nc.scalar.activation(out=zt_0[:], in_=zt_psum[0][:], func=ACT.Identity, bias=b2_col[:, 0:1])
-        zt_1 = const.tile([P, N_ROWS], F32)
-        nc.vector.tensor_scalar(
-            out=zt_1[:], in0=zt_psum[1][:], scalar1=b2_col[:, 1:2], scalar2=None, op0=ALU.add
-        )
-        zt = [zt_0, zt_1]
-
+        zt = [const.tile([P, N_ROWS], F32, name="zt%d" % m) for m in range(H1_TILES)]
         z_sb = const.tile([P, ROW_TILES, H1], F32)
-        for bank in range(2):
+        z_out = out_0.rearrange("(p i) j -> p i j", i=ROW_TILES)
+        for a in range(HALVES):
+            nc.scalar.activation(
+                out=zt[0][:, half_cols[a]],
+                in_=zt_psum[0][:, half_cols[a]],
+                func=ACT.Identity,
+                bias=b2_col[:, 0:1],
+            )
+            nc.vector.tensor_scalar(
+                out=zt[1][:, half_cols[a]],
+                in0=zt_psum[1][:, half_cols[a]],
+                scalar1=b2_col[:, 1:2],
+                scalar2=None,
+                op0=ALU.add,
+            )
             nc.vector.tensor_tensor(
-                out=z_sb[:, 2 * bank : 2 * bank + 2, :],
-                in0=z_psum[bank][:],
-                in1=b2_spread[:].unsqueeze(1).to_broadcast([P, 2, H1]),
+                out=z_sb[:, half_tiles[a], :],
+                in0=z_psum[a][:],
+                in1=b2_spread[:].unsqueeze(1).to_broadcast([P, TILES_PER_HALF, H1]),
                 op=ALU.add,
             )
-        nc.sync.dma_start(out=out_0.rearrange("(p i) j -> p i j", i=ROW_TILES), in_=z_sb[:])
+            nc.sync.dma_start(out=z_out[:, half_tiles[a], :], in_=z_sb[:, half_tiles[a], :])
 
         CLUSTER_SLOT = 32
-        cross = work_pool.tile([P, ROW_TILES, CLUSTER_SLOT], F32, tag="work")
+        cross = acc_pool.tile([P, ROW_TILES, CLUSTER_SLOT], F32, tag="acc0")
         for i in range(ROW_TILES):
-            for half in range(H1_TILES):
+            for m in range(H1_TILES):
                 nc.tensor.matmul(
                     out=cross[:, i, 0:N_CLUSTERS],
-                    lhsT=zt[half][:, P * i : P * (i + 1)],
-                    rhs=minus_2c[:, half, :],
-                    start=(half == 0),
-                    stop=(half == H1_TILES - 1),
+                    lhsT=zt[m][:, P * i : P * (i + 1)],
+                    rhs=minus_2c[:, m, :],
+                    start=(m == 0),
+                    stop=(m == H1_TILES - 1),
                 )
         z_norm = const.tile([P, ROW_TILES], F32)
         z_squared = const.tile([P, H1], F32)
@@ -333,31 +361,37 @@ def tile_lintrans_pa_k_kernel(tc, x, W1, b1, W2, b2, clusters, out_0, out_1):
             nc.scalar.activation(
                 out=z_squared[:], in_=z_sb[:, i, :], func=ACT.Square, accum_out=z_norm[:, i : i + 1]
             )
+
         q_shape = [P, ROW_TILES, N_CLUSTERS]
-        norms = const.tile(q_shape, F32)
-        nc.vector.tensor_tensor(
-            out=norms[:],
-            in0=c_norm_plus_1[:].unsqueeze(1).to_broadcast(q_shape),
-            in1=z_norm[:].unsqueeze(2).to_broadcast(q_shape),
-            op=ALU.add,
-        )
+        half_shape = [P, TILES_PER_HALF, N_CLUSTERS]
         one_plus_d2 = const.tile(q_shape, F32)
-        nc.vector.tensor_tensor(
-            out=one_plus_d2[:], in0=cross[:, :, 0:N_CLUSTERS], in1=norms[:], op=ALU.add
-        )
         t_kernel = const.tile(q_shape, F32)
-        nc.vector.reciprocal(out=t_kernel[:], in_=one_plus_d2[:])
         t_sum = const.tile([P, ROW_TILES], F32)
-        nc.vector.tensor_reduce(
-            out=t_sum[:], in_=t_kernel[:], axis=mybir.AxisListType.X, op=ALU.add
-        )
         t_sum_inverse = const.tile([P, ROW_TILES], F32)
-        nc.vector.reciprocal(out=t_sum_inverse[:], in_=t_sum[:])
         q_sb = const.tile(q_shape, F32)
-        nc.vector.tensor_tensor(
-            out=q_sb[:],
-            in0=t_kernel[:],
-            in1=t_sum_inverse[:].unsqueeze(2).to_broadcast(q_shape),
-            op=ALU.mult,
-        )
+        for a in range(HALVES):
+            tiles = half_tiles[a]
+            nc.vector.tensor_tensor(
+                out=one_plus_d2[:, tiles, :],
+                in0=c_norm_plus_1[:].unsqueeze(1).to_broadcast(half_shape),
+                in1=z_norm[:, tiles].unsqueeze(2).to_broadcast(half_shape),
+                op=ALU.add,
+            )
+            nc.vector.tensor_tensor(
+                out=one_plus_d2[:, tiles, :],
+                in0=cross[:, tiles, 0:N_CLUSTERS],
+                in1=one_plus_d2[:, tiles, :],
+                op=ALU.add,
+            )
+            nc.vector.reciprocal(out=t_kernel[:, tiles, :], in_=one_plus_d2[:, tiles, :])
+            nc.vector.tensor_reduce(
+                out=t_sum[:, tiles], in_=t_kernel[:, tiles, :], axis=mybir.AxisListType.X, op=ALU.add
+            )
+            nc.vector.reciprocal(out=t_sum_inverse[:, tiles], in_=t_sum[:, tiles])
+            nc.vector.tensor_tensor(
+                out=q_sb[:, tiles, :],
+                in0=t_kernel[:, tiles, :],
+                in1=t_sum_inverse[:, tiles].unsqueeze(2).to_broadcast(half_shape),
+                op=ALU.mult,
+            )
         nc.sync.dma_start(out=out_1.rearrange("(p i) k -> p i k", i=ROW_TILES), in_=q_sb[:])

@@ -24,8 +24,8 @@ WORDS = K_PASS // 2
 FLOPS = 2 * N_ROWS * D_IN * H0 + 2 * N_ROWS * H0 * H1 + 3 * N_ROWS * H1 * N_CLUSTERS
 
 LONG_CHUNK = 4
-TAPER = [1, 1, 2]
-CHUNKS = TAPER + [LONG_CHUNK] * ((PASSES - 2 * sum(TAPER)) // LONG_CHUNK) + TAPER[::-1]
+TAPER = [2, 1, 1]
+CHUNKS = [LONG_CHUNK] * ((PASSES - sum(TAPER)) // LONG_CHUNK) + TAPER
 assert sum(CHUNKS) == PASSES
 RAW_BUFS = 4
 RUNS_PER_DMA = 4

@@ -23,55 +23,73 @@ WORDS = K_PASS // 2
 
 FLOPS = 2 * N_ROWS * D_IN * H0 + 2 * N_ROWS * H0 * H1 + 3 * N_ROWS * H1 * N_CLUSTERS
 
-LONG_CHUNK = 4
-TAPER = [2, 1, 1]
-CHUNKS = [LONG_CHUNK] * ((PASSES - sum(TAPER)) // LONG_CHUNK) + TAPER
-assert sum(CHUNKS) == PASSES
-RAW_BUFS = 4
-RUNS_PER_DMA = 4
-
-LAG = 2
+X_CHUNKS = [2, 2] + [4] * 6 + [2, 2]
+W_CHUNKS = [2] * 15 + [1, 1]
+assert sum(X_CHUNKS) == sum(W_CHUNKS) == PASSES
+X_BUFS, W_BUFS = 4, 8
+LEAD = 3
 
 W_COLS_VECTOR = 320
+W_COLS_VECTOR_LATE = 256
 
 
 def tile_lintrans_pa_k_kernel(tc, x, W1, b1, W2, b2, clusters, out_0, out_1):
     nc = tc.nc
     with ExitStack() as ctx:
         const = ctx.enter_context(tc.tile_pool(name="const", bufs=1))
-        x_pool = ctx.enter_context(tc.tile_pool(name="x_pool", bufs=RAW_BUFS))
-        w_pool = ctx.enter_context(tc.tile_pool(name="w_pool", bufs=RAW_BUFS))
-        grouped_pool = ctx.enter_context(tc.tile_pool(name="grouped_pool", bufs=4))
-        code_pool = ctx.enter_context(tc.tile_pool(name="code_pool", bufs=4))
+        x_pool = ctx.enter_context(tc.tile_pool(name="x_pool", bufs=X_BUFS))
+        w_pool = ctx.enter_context(tc.tile_pool(name="w_pool", bufs=W_BUFS))
+        grouped_pool = ctx.enter_context(tc.tile_pool(name="grouped_pool", bufs=3))
+        x_code_pool = ctx.enter_context(tc.tile_pool(name="x_code_pool", bufs=10))
+        w_code_pool = ctx.enter_context(tc.tile_pool(name="w_code_pool", bufs=4))
         acc_pool = ctx.enter_context(tc.psum_pool(name="acc_pool", bufs=1))
         work_pool = ctx.enter_context(tc.psum_pool(name="work_pool", bufs=4))
         ctx.enter_context(tc.manual_schedule())
 
         x_rows = x.rearrange("(p i) k -> p i k", i=ROW_TILES)
         w_rows = W1.rearrange("(s p e) n -> p s (e n)", p=P, e=2)
-        chunk_first = [sum(CHUNKS[:c]) for c in range(len(CHUNKS))]
-        chunk_of_pass = [c for c in range(len(CHUNKS)) for repeat in range(CHUNKS[c])]
-        raw = {}
+        x_first = [sum(X_CHUNKS[:c]) for c in range(len(X_CHUNKS))]
+        w_first = [sum(W_CHUNKS[:c]) for c in range(len(W_CHUNKS))]
+        x_chunk_of_pass = [c for c in range(len(X_CHUNKS)) for repeat in range(X_CHUNKS[c])]
+        w_chunk_of_pass = [c for c in range(len(W_CHUNKS)) for repeat in range(W_CHUNKS[c])]
+        x_raw = {}
+        w_raw = {}
 
-        def load_chunk(c):
-            first, count = chunk_first[c], CHUNKS[c]
-            w_raw = w_pool.tile([P, 2 * LONG_CHUNK, 2 * H0], BF16)
-            x_raw = x_pool.tile([P, ROW_TILES, LONG_CHUNK * K_PASS], BF16)
-            for s in range(0, 2 * count, RUNS_PER_DMA):
-                runs = min(RUNS_PER_DMA, 2 * count - s)
-                nc.sync.dma_start(
-                    out=w_raw[:, s : s + runs, :],
-                    in_=w_rows[:, 2 * first + s : 2 * first + s + runs, :],
-                )
-                if s == 0:
-                    nc.sync.dma_start(
-                        out=x_raw[:, :, 0 : count * K_PASS],
-                        in_=x_rows[:, :, first * K_PASS : (first + count) * K_PASS],
-                    )
-            raw[c] = (x_raw, w_raw)
+        def load_x(c):
+            first, count = x_first[c], X_CHUNKS[c]
+            x_raw[c] = x_pool.tile([P, ROW_TILES, max(X_CHUNKS) * K_PASS], BF16, name="x_raw")
+            nc.sync.dma_start(
+                out=x_raw[c][:, :, 0 : count * K_PASS],
+                in_=x_rows[:, :, first * K_PASS : (first + count) * K_PASS],
+            )
 
-        for c in range(RAW_BUFS):
-            load_chunk(c)
+        def load_w(c):
+            first, count = w_first[c], W_CHUNKS[c]
+            w_raw[c] = w_pool.tile([P, 2 * max(W_CHUNKS), 2 * H0], BF16, name="w_raw")
+            nc.sync.dma_start(
+                out=w_raw[c][:, 0 : 2 * count, :],
+                in_=w_rows[:, 2 * first : 2 * (first + count), :],
+            )
+
+        loads = []
+        for c in range(len(X_CHUNKS)):
+            freed = x_first[c - X_BUFS + 1] - 1 if c >= X_BUFS else -1
+            loads.append((x_first[c] - LEAD, freed, "x", c))
+        for c in range(len(W_CHUNKS)):
+            freed = w_first[c - W_BUFS + 1] - 1 + LEAD if c >= W_BUFS else -1
+            loads.append((w_first[c], freed, "w", c))
+        loads = sorted(loads, key=lambda load: load[0])
+
+        def issue_loads(step):
+            while loads and loads[0][1] <= step:
+                place, freed, kind, c = loads[0]
+                loads.remove(loads[0])
+                if kind == "x":
+                    load_x(c)
+                else:
+                    load_w(c)
+
+        issue_loads(-1)
 
         ident = const.tile([P, P], F32)
         make_identity(nc, ident[:])
@@ -162,37 +180,38 @@ def tile_lintrans_pa_k_kernel(tc, x, W1, b1, W2, b2, clusters, out_0, out_1):
             PASSES // 2 + 1: spread_b2_and_centroid_norms,
         }
 
-        X_PART, W_PART = 0, N_ROWS
         grouped = {}
         transposed = {}
         codes = {}
-        acc = []
+        acc = [acc_pool.tile([P, N_ROWS], F32, name="acc%d" % m) for m in range(H0_TILES)]
 
-        def regroup_w(g):
-            c = chunk_of_pass[g]
-            local = g - chunk_first[c]
-            grouped[g] = grouped_pool.tile(
-                [P, (N_ROWS + H0) * PACK], BF16, align_bytes=64, name="grouped"
+        def new_grouped(kind, g):
+            grouped[kind, g] = grouped_pool.tile(
+                [P, N_ROWS * PACK], BF16, align_bytes=64, name="grouped_" + kind
             )
-            rows = raw[c][1][:, 2 * local : 2 * local + 2, :].rearrange(
+
+        def new_codes(kind, g):
+            pool = x_code_pool if kind == "x" else w_code_pool
+            words = pool.tile([P, N_ROWS], U32, align_bytes=64, name="words_" + kind)
+            scales = pool.tile([P, N_ROWS], U8, align_bytes=64, name="scales_" + kind)
+            codes[kind, g] = (words, scales)
+
+        def regroup_w(engine_copy, g, cols):
+            c = w_chunk_of_pass[g]
+            local = g - w_first[c]
+            rows = w_raw[c][:, 2 * local : 2 * local + 2, :].rearrange(
                 "p u (e n) -> p (u e) n", e=2
             )
-            words = grouped[g][:, W_PART * PACK :].rearrange("p (n t) -> p n t", t=PACK)
-            vector_cols = slice(0, W_COLS_VECTOR)
-            scalar_cols = slice(W_COLS_VECTOR, H0)
-            nc.vector.tensor_copy(
-                out=words[:, vector_cols, :].rearrange("p (c i) t -> p c t i", i=4),
-                in_=rows[:, :, vector_cols].rearrange("p t (c i) -> p c t i", i=4),
-            )
-            nc.scalar.copy(
-                out=words[:, scalar_cols, :].rearrange("p (c i) t -> p c t i", i=4),
-                in_=rows[:, :, scalar_cols].rearrange("p t (c i) -> p c t i", i=4),
+            words = grouped["w", g][:].rearrange("p (n t) -> p n t", t=PACK)
+            engine_copy(
+                out=words[:, cols, :].rearrange("p (c i) t -> p c t i", i=4),
+                in_=rows[:, :, cols].rearrange("p t (c i) -> p c t i", i=4),
             )
 
         def transpose_x(g):
-            c = chunk_of_pass[g]
-            local = g - chunk_first[c]
-            x_words = raw[c][0][:].bitcast(F32)
+            c = x_chunk_of_pass[g]
+            local = g - x_first[c]
+            x_words = x_raw[c][:].bitcast(F32)
             transposed[g] = []
             for bank in range(2):
                 turned = work_pool.tile([P, 2, 2 * P], F32, tag="work")
@@ -207,55 +226,74 @@ def tile_lintrans_pa_k_kernel(tc, x, W1, b1, W2, b2, clusters, out_0, out_1):
                 transposed[g].append(turned)
 
         def copy_x(g):
-            pairs = grouped[g][:].bitcast(F32)[:, 0 : N_ROWS * 2].rearrange(
-                "p (c u) -> p c u", u=2
-            )
+            pairs = grouped["x", g][:].bitcast(F32).rearrange("p (c u) -> p c u", u=2)
             for bank in range(2):
                 nc.scalar.copy(
                     out=pairs[:, 2 * P * bank : 2 * P * (bank + 1), :],
                     in_=transposed[g][bank][:].rearrange("p u c -> p c u"),
                 )
 
-        def quantise(g):
-            words = code_pool.tile([P, N_ROWS + H0], U32, align_bytes=64, name="words")
-            scales = code_pool.tile([P, N_ROWS + H0], U8, align_bytes=64, name="scales")
-            nc.vector.quantize_mx(out=words[:].bitcast(FP8X4), scales=scales[:], in_=grouped[g][:])
-            codes[g] = (words, scales)
+        def quantise(kind, g, cols):
+            words, scales = codes[kind, g]
+            nc.vector.quantize_mx(
+                out=words[:, cols].bitcast(FP8X4),
+                scales=scales[:, cols],
+                in_=grouped[kind, g][:, PACK * cols.start : PACK * cols.stop],
+            )
 
-        def multiply(g):
-            words, scales = codes[g]
-            for m in range(H0_TILES):
-                if g == 0:
-                    acc.append(acc_pool.tile([P, N_ROWS], F32, name="acc%d" % m))
-                w_cols = slice(W_PART + P * m, W_PART + P * (m + 1))
-                x_cols = slice(X_PART, X_PART + N_ROWS)
-                nc.tensor.matmul_mx(
-                    out=acc[m][:],
-                    lhsT=words[:, w_cols].bitcast(FP8X4),
-                    lhsT_scale=scales[:, w_cols],
-                    rhs=words[:, x_cols].bitcast(FP8X4),
-                    rhs_scale=scales[:, x_cols],
-                    start=(g == 0),
-                    stop=(g == PASSES - 1),
-                )
+        def multiply(g, m):
+            x_words, x_scales = codes["x", g]
+            w_words, w_scales = codes["w", g]
+            w_cols = slice(P * m, P * (m + 1))
+            nc.tensor.matmul_mx(
+                out=acc[m][:],
+                lhsT=w_words[:, w_cols].bitcast(FP8X4),
+                lhsT_scale=w_scales[:, w_cols],
+                rhs=x_words[:].bitcast(FP8X4),
+                rhs_scale=x_scales[:],
+                start=(g == 0),
+                stop=(g == PASSES - 1),
+            )
 
-        regroup_w(0)
-        for step in range(PASSES + LAG):
+        ALL = slice(0, N_ROWS)
+
+        last = PASSES - 1
+        for step in range(last + LEAD + 2):
             if step < PASSES:
+                new_grouped("x", step)
                 transpose_x(step)
                 copy_x(step)
-                c = chunk_of_pass[step]
-                is_last_of_chunk = step + 1 == chunk_first[c] + CHUNKS[c]
-                if is_last_of_chunk and c + RAW_BUFS < len(CHUNKS):
-                    load_chunk(c + RAW_BUFS)
+            g = step - LEAD
+            if 0 <= g < last:
+                new_grouped("w", g)
+                cut = W_COLS_VECTOR if step < PASSES else W_COLS_VECTOR_LATE
+                regroup_w(nc.vector.tensor_copy, g, slice(0, cut))
+                regroup_w(nc.scalar.copy, g, slice(cut, H0))
+            issue_loads(step)
             if step in small_work:
                 small_work[step]()
-            if step + 1 < PASSES:
-                regroup_w(step + 1)
-            if step < PASSES:
-                quantise(step)
-            if step >= LAG:
-                multiply(step - LAG)
+            if 1 <= step <= PASSES:
+                new_codes("x", step - 1)
+                quantise("x", step - 1, ALL)
+            if 0 <= g - 1 < last:
+                new_codes("w", g - 1)
+                quantise("w", g - 1, ALL)
+            if 0 <= g - 2 < last:
+                for m in range(H0_TILES):
+                    multiply(g - 2, m)
+
+        w_tile = [slice(P * m, P * (m + 1)) for m in range(H0_TILES)]
+        new_grouped("w", last)
+        new_codes("w", last)
+        regroup_w(nc.scalar.copy, last, w_tile[3])
+        regroup_w(nc.vector.tensor_copy, last, w_tile[0])
+        regroup_w(nc.vector.tensor_copy, last, w_tile[1])
+        quantise("w", last, w_tile[0])
+        regroup_w(nc.vector.tensor_copy, last, w_tile[2])
+        for m in range(1, H0_TILES):
+            quantise("w", last, w_tile[m])
+        for m in range(H0_TILES):
+            multiply(last, m)
 
         HALVES = 2
         HALF = N_ROWS // HALVES
@@ -264,14 +302,21 @@ def tile_lintrans_pa_k_kernel(tc, x, W1, b1, W2, b2, clusters, out_0, out_1):
         half_tiles = [slice(TILES_PER_HALF * a, TILES_PER_HALF * (a + 1)) for a in range(HALVES)]
 
         h_planes = const.tile([P, PACK, N_ROWS], BF16)
+
+        def silu(m, cols):
+            nc.scalar.activation(
+                out=h_planes[:, m, cols],
+                in_=acc[m][:, cols],
+                func=ACT.Silu,
+                bias=b1_col[:, m : m + 1],
+            )
+
+        for m in range(2):
+            silu(m, ALL)
         for a in range(HALVES):
-            for m in range(H0_TILES):
-                nc.scalar.activation(
-                    out=h_planes[:, m, half_cols[a]],
-                    in_=acc[m][:, half_cols[a]],
-                    func=ACT.Silu,
-                    bias=b1_col[:, m : m + 1],
-                )
+            for m in range(2, H0_TILES):
+                silu(m, half_cols[a])
+
         h_grouped = const.tile([P, N_ROWS, PACK], BF16, align_bytes=64)
         h_codes = const.tile([P, N_ROWS], U32, align_bytes=64)
         h_scales = const.tile([P, N_ROWS], U8, align_bytes=64)
@@ -286,19 +331,14 @@ def tile_lintrans_pa_k_kernel(tc, x, W1, b1, W2, b2, clusters, out_0, out_1):
                 in_=h_grouped[:, half_cols[a], :].rearrange("p c t -> p (c t)"),
             )
 
-        zt_psum = [
-            work_pool.tile([P, N_ROWS], F32, tag="work", name="zt_psum%d" % m)
-            for m in range(H1_TILES)
-        ]
-        z_psum = [
-            work_pool.tile([P, TILES_PER_HALF, H1], F32, tag="work", name="z_psum%d" % a)
-            for a in range(HALVES)
-        ]
+        zt_psum = {}
+        z_psum = {}
         for a in range(HALVES):
             for m in range(H1_TILES):
+                zt_psum[a, m] = work_pool.tile([P, HALF], F32, tag="work", name="zt_psum")
                 j_cols = slice(P * m, P * (m + 1))
                 nc.tensor.matmul_mx(
-                    out=zt_psum[m][:, half_cols[a]],
+                    out=zt_psum[a, m][:],
                     lhsT=w2_codes[:, j_cols].bitcast(FP8X4),
                     lhsT_scale=w2_scales[:, j_cols],
                     rhs=h_codes[:, half_cols[a]].bitcast(FP8X4),
@@ -306,6 +346,7 @@ def tile_lintrans_pa_k_kernel(tc, x, W1, b1, W2, b2, clusters, out_0, out_1):
                     start=True,
                     stop=True,
                 )
+            z_psum[a] = acc_pool.tile([P, TILES_PER_HALF, H1], F32, tag="acc%d" % a, name="z_psum")
             for j in range(TILES_PER_HALF):
                 i = TILES_PER_HALF * a + j
                 row_cols = slice(P * i, P * (i + 1))
@@ -319,23 +360,38 @@ def tile_lintrans_pa_k_kernel(tc, x, W1, b1, W2, b2, clusters, out_0, out_1):
                     stop=True,
                 )
 
-        zt = [const.tile([P, N_ROWS], F32, name="zt%d" % m) for m in range(H1_TILES)]
+        CLUSTER_SLOT = 32
+        q_shape = [P, ROW_TILES, N_CLUSTERS]
+        zt = const.tile([P, H1_TILES, N_ROWS], F32)
         z_sb = const.tile([P, ROW_TILES, H1], F32)
+        z_squared = const.tile([P, H1], F32)
+        z_norm = const.tile([P, ROW_TILES], F32)
+        norms = const.tile(q_shape, F32)
+        cross = acc_pool.tile([P, ROW_TILES, CLUSTER_SLOT], F32, tag="acc2")
         z_out = out_0.rearrange("(p i) j -> p i j", i=ROW_TILES)
         for a in range(HALVES):
             nc.scalar.activation(
-                out=zt[0][:, half_cols[a]],
-                in_=zt_psum[0][:, half_cols[a]],
+                out=zt[:, 0, half_cols[a]],
+                in_=zt_psum[a, 0][:],
                 func=ACT.Identity,
                 bias=b2_col[:, 0:1],
             )
             nc.vector.tensor_scalar(
-                out=zt[1][:, half_cols[a]],
-                in0=zt_psum[1][:, half_cols[a]],
+                out=zt[:, 1, half_cols[a]],
+                in0=zt_psum[a, 1][:],
                 scalar1=b2_col[:, 1:2],
                 scalar2=None,
                 op0=ALU.add,
             )
+            for i in range(TILES_PER_HALF * a, TILES_PER_HALF * (a + 1)):
+                for m in range(H1_TILES):
+                    nc.tensor.matmul(
+                        out=cross[:, i, 0:N_CLUSTERS],
+                        lhsT=zt[:, m, P * i : P * (i + 1)],
+                        rhs=minus_2c[:, m, :],
+                        start=(m == 0),
+                        stop=(m == H1_TILES - 1),
+                    )
             nc.vector.tensor_tensor(
                 out=z_sb[:, half_tiles[a], :],
                 in0=z_psum[a][:],
@@ -343,55 +399,37 @@ def tile_lintrans_pa_k_kernel(tc, x, W1, b1, W2, b2, clusters, out_0, out_1):
                 op=ALU.add,
             )
             nc.sync.dma_start(out=z_out[:, half_tiles[a], :], in_=z_sb[:, half_tiles[a], :])
-
-        CLUSTER_SLOT = 32
-        cross = acc_pool.tile([P, ROW_TILES, CLUSTER_SLOT], F32, tag="acc0")
-        for i in range(ROW_TILES):
-            for m in range(H1_TILES):
-                nc.tensor.matmul(
-                    out=cross[:, i, 0:N_CLUSTERS],
-                    lhsT=zt[m][:, P * i : P * (i + 1)],
-                    rhs=minus_2c[:, m, :],
-                    start=(m == 0),
-                    stop=(m == H1_TILES - 1),
+            for i in range(TILES_PER_HALF * a, TILES_PER_HALF * (a + 1)):
+                nc.scalar.activation(
+                    out=z_squared[:],
+                    in_=z_sb[:, i, :],
+                    func=ACT.Square,
+                    accum_out=z_norm[:, i : i + 1],
                 )
-        z_norm = const.tile([P, ROW_TILES], F32)
-        z_squared = const.tile([P, H1], F32)
-        for i in range(ROW_TILES):
-            nc.scalar.activation(
-                out=z_squared[:], in_=z_sb[:, i, :], func=ACT.Square, accum_out=z_norm[:, i : i + 1]
-            )
+        nc.vector.tensor_tensor(
+            out=norms[:],
+            in0=c_norm_plus_1[:].unsqueeze(1).to_broadcast(q_shape),
+            in1=z_norm[:].unsqueeze(2).to_broadcast(q_shape),
+            op=ALU.add,
+        )
 
-        q_shape = [P, ROW_TILES, N_CLUSTERS]
-        half_shape = [P, TILES_PER_HALF, N_CLUSTERS]
         one_plus_d2 = const.tile(q_shape, F32)
         t_kernel = const.tile(q_shape, F32)
         t_sum = const.tile([P, ROW_TILES], F32)
         t_sum_inverse = const.tile([P, ROW_TILES], F32)
         q_sb = const.tile(q_shape, F32)
-        for a in range(HALVES):
-            tiles = half_tiles[a]
-            nc.vector.tensor_tensor(
-                out=one_plus_d2[:, tiles, :],
-                in0=c_norm_plus_1[:].unsqueeze(1).to_broadcast(half_shape),
-                in1=z_norm[:, tiles].unsqueeze(2).to_broadcast(half_shape),
-                op=ALU.add,
-            )
-            nc.vector.tensor_tensor(
-                out=one_plus_d2[:, tiles, :],
-                in0=cross[:, tiles, 0:N_CLUSTERS],
-                in1=one_plus_d2[:, tiles, :],
-                op=ALU.add,
-            )
-            nc.vector.reciprocal(out=t_kernel[:, tiles, :], in_=one_plus_d2[:, tiles, :])
-            nc.vector.tensor_reduce(
-                out=t_sum[:, tiles], in_=t_kernel[:, tiles, :], axis=mybir.AxisListType.X, op=ALU.add
-            )
-            nc.vector.reciprocal(out=t_sum_inverse[:, tiles], in_=t_sum[:, tiles])
-            nc.vector.tensor_tensor(
-                out=q_sb[:, tiles, :],
-                in0=t_kernel[:, tiles, :],
-                in1=t_sum_inverse[:, tiles].unsqueeze(2).to_broadcast(half_shape),
-                op=ALU.mult,
-            )
+        nc.vector.tensor_tensor(
+            out=one_plus_d2[:], in0=cross[:, :, 0:N_CLUSTERS], in1=norms[:], op=ALU.add
+        )
+        nc.vector.reciprocal(out=t_kernel[:], in_=one_plus_d2[:])
+        nc.vector.tensor_reduce(
+            out=t_sum[:], in_=t_kernel[:], axis=mybir.AxisListType.X, op=ALU.add
+        )
+        nc.vector.reciprocal(out=t_sum_inverse[:], in_=t_sum[:])
+        nc.vector.tensor_tensor(
+            out=q_sb[:],
+            in0=t_kernel[:],
+            in1=t_sum_inverse[:].unsqueeze(2).to_broadcast(q_shape),
+            op=ALU.mult,
+        )
         nc.sync.dma_start(out=out_1.rearrange("(p i) k -> p i k", i=ROW_TILES), in_=q_sb[:])

@@ -47,7 +47,7 @@ def tile_lintrans_pa_k_kernel(tc, x, W1, b1, W2, b2, clusters, out_0, out_1):
         ctx.enter_context(tc.manual_schedule())
 
         x_rows = x.rearrange("(p i) k -> p i k", i=ROW_TILES)
-        w_rows = W1.rearrange("(s p e) n -> p s (e n)", p=P, e=2)
+        w_rows = W1.rearrange("(g p t) n -> p g (t n)", p=P, t=PACK)
         x_first = [sum(X_CHUNKS[:c]) for c in range(len(X_CHUNKS))]
         w_first = [sum(W_CHUNKS[:c]) for c in range(len(W_CHUNKS))]
         x_chunk_of_pass = [c for c in range(len(X_CHUNKS)) for repeat in range(X_CHUNKS[c])]
@@ -65,10 +65,9 @@ def tile_lintrans_pa_k_kernel(tc, x, W1, b1, W2, b2, clusters, out_0, out_1):
 
         def load_w(c):
             first, count = w_first[c], W_CHUNKS[c]
-            w_raw[c] = w_pool.tile([P, 2 * max(W_CHUNKS), 2 * H0], BF16, name="w_raw")
+            w_raw[c] = w_pool.tile([P, max(W_CHUNKS), PACK * H0], BF16, name="w_raw")
             nc.sync.dma_start(
-                out=w_raw[c][:, 0 : 2 * count, :],
-                in_=w_rows[:, 2 * first : 2 * (first + count), :],
+                out=w_raw[c][:, 0:count, :], in_=w_rows[:, first : first + count, :]
             )
 
         loads = []
@@ -127,19 +126,36 @@ def tile_lintrans_pa_k_kernel(tc, x, W1, b1, W2, b2, clusters, out_0, out_1):
         w2_codes = const.tile([P, H1], U32, align_bytes=64)
         w2_scales = const.tile([P, H1], U8, align_bytes=64)
 
-        def turn_small_rows_into_columns():
-            small_rows_f32 = const.tile([P, P], F32)
+        small_rows_f32 = const.tile([P, P], F32)
+        w2_grouped = const.tile([P, H1, PACK], BF16, align_bytes=64)
+        small_psum = {}
+
+        def widen_small_rows():
             nc.vector.tensor_copy(out=small_rows_f32[:], in_=small_rows[:])
-            turned = work_pool.tile([P, P], F32, tag="work")
-            nc.tensor.transpose(turned[:], small_rows_f32[:], ident[:])
-            nc.vector.tensor_copy(out=small_cols[:], in_=turned[:])
+            nc.vector.tensor_copy(
+                out=w2_grouped[:].rearrange("p (c i) t -> p c t i", i=4),
+                in_=w2_raw[:].rearrange("p t (c i) -> p c t i", i=4),
+            )
+
+        def turn_small_rows_into_columns():
+            small_psum["turned"] = work_pool.tile([P, P], F32, tag="work", name="turned")
+            nc.tensor.transpose(small_psum["turned"][:], small_rows_f32[:], ident[:])
+            nc.vector.quantize_mx(
+                out=w2_codes[:].bitcast(FP8X4),
+                scales=w2_scales[:],
+                in_=w2_grouped[:].rearrange("p j t -> p (j t)"),
+            )
+            nc.scalar.copy(out=small_cols[:], in_=small_psum["turned"][:])
+
+        def prepare_centroids():
             nc.vector.tensor_scalar(
                 out=minus_2c[:], in0=clusters_t, scalar1=-2.0, scalar2=None, op0=ALU.mult
             )
             nc.vector.tensor_tensor(out=c_squared[:], in0=clusters_t, in1=clusters_t, op=ALU.mult)
 
         def spread_b2_and_centroid_norms():
-            spread = work_pool.tile([P, 2 * H1], F32, tag="work")
+            spread = work_pool.tile([P, 2 * H1], F32, tag="work", name="spread")
+            small_psum["spread"] = spread
             for half in range(H1_TILES):
                 nc.tensor.matmul(
                     out=spread[:, P * half : P * (half + 1)],
@@ -156,28 +172,23 @@ def tile_lintrans_pa_k_kernel(tc, x, W1, b1, W2, b2, clusters, out_0, out_1):
                     start=(half == 0),
                     stop=(half == H1_TILES - 1),
                 )
-            nc.vector.tensor_copy(out=b2_spread[:], in_=spread[:, 0:H1])
+            nc.scalar.copy(out=b2_spread[:], in_=spread[:, 0:H1])
+
+        def add_1_to_centroid_norms():
             nc.vector.tensor_scalar(
                 out=c_norm_plus_1[:],
-                in0=spread[:, H1 : H1 + N_CLUSTERS],
+                in0=small_psum["spread"][:, H1 : H1 + N_CLUSTERS],
                 scalar1=1.0,
                 scalar2=None,
                 op0=ALU.add,
             )
-            w2_grouped = const.tile([P, H1, PACK], BF16, align_bytes=64)
-            nc.vector.tensor_copy(
-                out=w2_grouped[:].rearrange("p (c i) t -> p c t i", i=4),
-                in_=w2_raw[:].rearrange("p t (c i) -> p c t i", i=4),
-            )
-            nc.vector.quantize_mx(
-                out=w2_codes[:].bitcast(FP8X4),
-                scales=w2_scales[:],
-                in_=w2_grouped[:].rearrange("p j t -> p (j t)"),
-            )
 
         small_work = {
-            PASSES // 2: turn_small_rows_into_columns,
-            PASSES // 2 + 1: spread_b2_and_centroid_norms,
+            PASSES // 2: widen_small_rows,
+            PASSES // 2 + 1: turn_small_rows_into_columns,
+            PASSES // 2 + 2: prepare_centroids,
+            PASSES // 2 + 3: spread_b2_and_centroid_norms,
+            PASSES // 2 + 4: add_1_to_centroid_norms,
         }
 
         grouped = {}
@@ -199,9 +210,7 @@ def tile_lintrans_pa_k_kernel(tc, x, W1, b1, W2, b2, clusters, out_0, out_1):
         def regroup_w(engine_copy, g, cols):
             c = w_chunk_of_pass[g]
             local = g - w_first[c]
-            rows = w_raw[c][:, 2 * local : 2 * local + 2, :].rearrange(
-                "p u (e n) -> p (u e) n", e=2
-            )
+            rows = w_raw[c][:, local, :].rearrange("p (t n) -> p t n", t=PACK)
             words = grouped["w", g][:].rearrange("p (n t) -> p n t", t=PACK)
             engine_copy(
                 out=words[:, cols, :].rearrange("p (c i) t -> p c t i", i=4),
@@ -217,10 +226,9 @@ def tile_lintrans_pa_k_kernel(tc, x, W1, b1, W2, b2, clusters, out_0, out_1):
                 turned = work_pool.tile([P, 2, 2 * P], F32, tag="work")
                 for u in range(2):
                     for j in range(2):
-                        first_word = WORDS * local + P * u
                         nc.tensor.transpose(
                             turned[:, u, P * j : P * (j + 1)],
-                            x_words[:, 2 * bank + j, first_word : first_word + P],
+                            x_words[:, 2 * bank + j, WORDS * local + u : WORDS * (local + 1) : 2],
                             ident[:],
                         )
                 transposed[g].append(turned)
@@ -259,9 +267,11 @@ def tile_lintrans_pa_k_kernel(tc, x, W1, b1, W2, b2, clusters, out_0, out_1):
 
         last = PASSES - 1
         for step in range(last + LEAD + 2):
+            if step < PASSES and step % 2 == 0:
+                transpose_x(step)
+                transpose_x(step + 1)
             if step < PASSES:
                 new_grouped("x", step)
-                transpose_x(step)
                 copy_x(step)
             g = step - LEAD
             if 0 <= g < last:
@@ -295,11 +305,10 @@ def tile_lintrans_pa_k_kernel(tc, x, W1, b1, W2, b2, clusters, out_0, out_1):
         for m in range(H0_TILES):
             multiply(last, m)
 
-        HALVES = 2
-        HALF = N_ROWS // HALVES
-        TILES_PER_HALF = ROW_TILES // HALVES
-        half_cols = [slice(HALF * a, HALF * (a + 1)) for a in range(HALVES)]
-        half_tiles = [slice(TILES_PER_HALF * a, TILES_PER_HALF * (a + 1)) for a in range(HALVES)]
+        PART_TILES = [[0], [1], [2, 3]]
+        PARTS = len(PART_TILES)
+        part_cols = [slice(P * t[0], P * (t[-1] + 1)) for t in PART_TILES]
+        part_tiles = [slice(t[0], t[-1] + 1) for t in PART_TILES]
 
         h_planes = const.tile([P, PACK, N_ROWS], BF16)
 
@@ -311,47 +320,53 @@ def tile_lintrans_pa_k_kernel(tc, x, W1, b1, W2, b2, clusters, out_0, out_1):
                 bias=b1_col[:, m : m + 1],
             )
 
-        for m in range(2):
-            silu(m, ALL)
-        for a in range(HALVES):
-            for m in range(2, H0_TILES):
-                silu(m, half_cols[a])
+        for a in range(PARTS):
+            for m in range(H0_TILES):
+                silu(m, part_cols[a])
 
         h_grouped = const.tile([P, N_ROWS, PACK], BF16, align_bytes=64)
         h_codes = const.tile([P, N_ROWS], U32, align_bytes=64)
         h_scales = const.tile([P, N_ROWS], U8, align_bytes=64)
-        for a in range(HALVES):
+
+        def regroup_h(a):
             nc.vector.tensor_copy(
-                out=h_grouped[:, half_cols[a], :].rearrange("p (c i) t -> p c t i", i=4),
-                in_=h_planes[:, :, half_cols[a]].rearrange("p t (c i) -> p c t i", i=4),
+                out=h_grouped[:, part_cols[a], :].rearrange("p (c i) t -> p c t i", i=4),
+                in_=h_planes[:, :, part_cols[a]].rearrange("p t (c i) -> p c t i", i=4),
             )
+
+        def quantise_h(a):
             nc.vector.quantize_mx(
-                out=h_codes[:, half_cols[a]].bitcast(FP8X4),
-                scales=h_scales[:, half_cols[a]],
-                in_=h_grouped[:, half_cols[a], :].rearrange("p c t -> p (c t)"),
+                out=h_codes[:, part_cols[a]].bitcast(FP8X4),
+                scales=h_scales[:, part_cols[a]],
+                in_=h_grouped[:, part_cols[a], :].rearrange("p c t -> p (c t)"),
             )
 
         zt_psum = {}
         z_psum = {}
-        for a in range(HALVES):
+        Z_BANK = ["acc0", "acc2", "acc3"]
+
+        def second_matmul(a):
             for m in range(H1_TILES):
-                zt_psum[a, m] = work_pool.tile([P, HALF], F32, tag="work", name="zt_psum")
+                zt_psum[a, m] = work_pool.tile(
+                    [P, P * len(PART_TILES[a])], F32, tag="work", name="zt_psum"
+                )
                 j_cols = slice(P * m, P * (m + 1))
                 nc.tensor.matmul_mx(
                     out=zt_psum[a, m][:],
                     lhsT=w2_codes[:, j_cols].bitcast(FP8X4),
                     lhsT_scale=w2_scales[:, j_cols],
-                    rhs=h_codes[:, half_cols[a]].bitcast(FP8X4),
-                    rhs_scale=h_scales[:, half_cols[a]],
+                    rhs=h_codes[:, part_cols[a]].bitcast(FP8X4),
+                    rhs_scale=h_scales[:, part_cols[a]],
                     start=True,
                     stop=True,
                 )
-            z_psum[a] = acc_pool.tile([P, TILES_PER_HALF, H1], F32, tag="acc%d" % a, name="z_psum")
-            for j in range(TILES_PER_HALF):
-                i = TILES_PER_HALF * a + j
+            z_psum[a] = acc_pool.tile(
+                [P, len(PART_TILES[a]), H1], F32, tag=Z_BANK[a], name="z_psum"
+            )
+            for i in PART_TILES[a]:
                 row_cols = slice(P * i, P * (i + 1))
                 nc.tensor.matmul_mx(
-                    out=z_psum[a][:, j, :],
+                    out=z_psum[a][:, i - PART_TILES[a][0], :],
                     lhsT=h_codes[:, row_cols].bitcast(FP8X4),
                     lhsT_scale=h_scales[:, row_cols],
                     rhs=w2_codes[:].bitcast(FP8X4),
@@ -367,64 +382,115 @@ def tile_lintrans_pa_k_kernel(tc, x, W1, b1, W2, b2, clusters, out_0, out_1):
         z_squared = const.tile([P, H1], F32)
         z_norm = const.tile([P, ROW_TILES], F32)
         norms = const.tile(q_shape, F32)
-        cross = acc_pool.tile([P, ROW_TILES, CLUSTER_SLOT], F32, tag="acc2")
+        cross = {}
         z_out = out_0.rearrange("(p i) j -> p i j", i=ROW_TILES)
-        for a in range(HALVES):
+
+        def zt_by_scalar(a, m):
             nc.scalar.activation(
-                out=zt[:, 0, half_cols[a]],
-                in_=zt_psum[a, 0][:],
+                out=zt[:, m, part_cols[a]],
+                in_=zt_psum[a, m][:],
                 func=ACT.Identity,
-                bias=b2_col[:, 0:1],
+                bias=b2_col[:, m : m + 1],
             )
+
+        def zt_by_vector(a, m):
             nc.vector.tensor_scalar(
-                out=zt[:, 1, half_cols[a]],
-                in0=zt_psum[a, 1][:],
-                scalar1=b2_col[:, 1:2],
+                out=zt[:, m, part_cols[a]],
+                in0=zt_psum[a, m][:],
+                scalar1=b2_col[:, m : m + 1],
                 scalar2=None,
                 op0=ALU.add,
             )
-            for i in range(TILES_PER_HALF * a, TILES_PER_HALF * (a + 1)):
+
+        def cross_term(a):
+            if a == 0:
+                cross[0] = acc_pool.tile([P, 2, CLUSTER_SLOT], F32, tag="acc1", name="cross_early")
+            if a == 2:
+                cross[1] = work_pool.tile([P, 2, CLUSTER_SLOT], F32, tag="work", name="cross_late")
+            for i in PART_TILES[a]:
                 for m in range(H1_TILES):
                     nc.tensor.matmul(
-                        out=cross[:, i, 0:N_CLUSTERS],
+                        out=cross[i // 2][:, i % 2, 0:N_CLUSTERS],
                         lhsT=zt[:, m, P * i : P * (i + 1)],
                         rhs=minus_2c[:, m, :],
                         start=(m == 0),
                         stop=(m == H1_TILES - 1),
                     )
+
+        def add_b2(a):
             nc.vector.tensor_tensor(
-                out=z_sb[:, half_tiles[a], :],
+                out=z_sb[:, part_tiles[a], :],
                 in0=z_psum[a][:],
-                in1=b2_spread[:].unsqueeze(1).to_broadcast([P, TILES_PER_HALF, H1]),
+                in1=b2_spread[:].unsqueeze(1).to_broadcast([P, len(PART_TILES[a]), H1]),
                 op=ALU.add,
             )
-            nc.sync.dma_start(out=z_out[:, half_tiles[a], :], in_=z_sb[:, half_tiles[a], :])
-            for i in range(TILES_PER_HALF * a, TILES_PER_HALF * (a + 1)):
+            nc.sync.dma_start(out=z_out[:, part_tiles[a], :], in_=z_sb[:, part_tiles[a], :])
+
+        def square_z(a):
+            for i in PART_TILES[a]:
                 nc.scalar.activation(
                     out=z_squared[:],
                     in_=z_sb[:, i, :],
                     func=ACT.Square,
                     accum_out=z_norm[:, i : i + 1],
                 )
-        nc.vector.tensor_tensor(
-            out=norms[:],
-            in0=c_norm_plus_1[:].unsqueeze(1).to_broadcast(q_shape),
-            in1=z_norm[:].unsqueeze(2).to_broadcast(q_shape),
-            op=ALU.add,
-        )
+
+        regroup_h(0)
+        quantise_h(0)
+        second_matmul(0)
+        regroup_h(1)
+        quantise_h(1)
+        second_matmul(1)
+        zt_by_scalar(0, 0)
+        zt_by_vector(0, 1)
+        cross_term(0)
+        regroup_h(2)
+        zt_by_scalar(1, 0)
+        zt_by_vector(1, 1)
+        quantise_h(2)
+        second_matmul(2)
+        cross_term(1)
+        add_b2(0)
+        add_b2(1)
+        square_z(0)
+        zt_by_scalar(2, 0)
+        zt_by_vector(2, 1)
+        cross_term(2)
+        add_b2(2)
+        square_z(1)
+        square_z(2)
 
         one_plus_d2 = const.tile(q_shape, F32)
         t_kernel = const.tile(q_shape, F32)
         t_sum = const.tile([P, ROW_TILES], F32)
         t_sum_inverse = const.tile([P, ROW_TILES], F32)
         q_sb = const.tile(q_shape, F32)
-        nc.vector.tensor_tensor(
-            out=one_plus_d2[:], in0=cross[:, :, 0:N_CLUSTERS], in1=norms[:], op=ALU.add
-        )
-        nc.vector.reciprocal(out=t_kernel[:], in_=one_plus_d2[:])
-        nc.vector.tensor_reduce(
-            out=t_sum[:], in_=t_kernel[:], axis=mybir.AxisListType.X, op=ALU.add
-        )
+
+        def add_norms(tiles, shape):
+            nc.vector.tensor_tensor(
+                out=norms[:, tiles, :],
+                in0=c_norm_plus_1[:].unsqueeze(1).to_broadcast(shape),
+                in1=z_norm[:, tiles].unsqueeze(2).to_broadcast(shape),
+                op=ALU.add,
+            )
+
+        def kernel_of_distances(tiles):
+            nc.vector.tensor_tensor(
+                out=one_plus_d2[:, tiles, :],
+                in0=cross[tiles.start // 2][:, :, 0:N_CLUSTERS],
+                in1=norms[:, tiles, :],
+                op=ALU.add,
+            )
+            nc.vector.reciprocal(out=t_kernel[:, tiles, :], in_=one_plus_d2[:, tiles, :])
+            nc.vector.tensor_reduce(
+                out=t_sum[:, tiles], in_=t_kernel[:, tiles, :], axis=mybir.AxisListType.X, op=ALU.add
+            )
+
+        early, late = slice(0, 2), slice(2, ROW_TILES)
+        pair_shape = [P, 2, N_CLUSTERS]
+        for tiles in [early, late]:
+            add_norms(tiles, pair_shape)
+            kernel_of_distances(tiles)
         nc.vector.reciprocal(out=t_sum_inverse[:], in_=t_sum[:])
         nc.vector.tensor_tensor(
             out=q_sb[:],

@@ -24,7 +24,7 @@ WORDS = K_PASS // 2
 FLOPS = 2 * N_ROWS * D_IN * H0 + 2 * N_ROWS * H0 * H1 + 3 * N_ROWS * H1 * N_CLUSTERS
 
 X_CHUNKS = [2, 2] + [4] * 6 + [2, 2]
-W_CHUNKS = [2] * 15 + [1, 1]
+W_CHUNKS = [2] * 12 + [1] * 8
 assert sum(X_CHUNKS) == sum(W_CHUNKS) == PASSES
 X_BUFS, W_BUFS = 4, 8
 LEAD = 3

@@ -23,14 +23,15 @@ WORDS = K_PASS // 2
 
 FLOPS = 2 * N_ROWS * D_IN * H0 + 2 * N_ROWS * H0 * H1 + 3 * N_ROWS * H1 * N_CLUSTERS
 
-X_CHUNKS = [2, 2] + [4] * 6 + [2, 2]
-W_CHUNKS = [2] * 12 + [1] * 8
+X_CHUNKS = [1, 1, 2, 2, 2] + [4] * 5 + [2, 2]
+W_CHUNKS = [1] * 4 + [2] * 12 + [1] * 4
 assert sum(X_CHUNKS) == sum(W_CHUNKS) == PASSES
 X_BUFS, W_BUFS = 4, 8
-LEAD = 3
+LEAD = 1
+
+X_AHEAD = 1.5
 
 W_COLS_VECTOR = 320
-W_COLS_VECTOR_LATE = 256
 
 
 def tile_lintrans_pa_k_kernel(tc, x, W1, b1, W2, b2, clusters, out_0, out_1):
@@ -40,14 +41,13 @@ def tile_lintrans_pa_k_kernel(tc, x, W1, b1, W2, b2, clusters, out_0, out_1):
         x_pool = ctx.enter_context(tc.tile_pool(name="x_pool", bufs=X_BUFS))
         w_pool = ctx.enter_context(tc.tile_pool(name="w_pool", bufs=W_BUFS))
         grouped_pool = ctx.enter_context(tc.tile_pool(name="grouped_pool", bufs=3))
-        x_code_pool = ctx.enter_context(tc.tile_pool(name="x_code_pool", bufs=10))
-        w_code_pool = ctx.enter_context(tc.tile_pool(name="w_code_pool", bufs=4))
+        code_pool = ctx.enter_context(tc.tile_pool(name="code_pool", bufs=6))
         acc_pool = ctx.enter_context(tc.psum_pool(name="acc_pool", bufs=1))
         work_pool = ctx.enter_context(tc.psum_pool(name="work_pool", bufs=4))
         ctx.enter_context(tc.manual_schedule())
 
         x_rows = x.rearrange("(p i) k -> p i k", i=ROW_TILES)
-        w_rows = W1.rearrange("(g p t) n -> p g (t n)", p=P, t=PACK)
+        w_rows = W1.rearrange("(s p e) n -> p s (e n)", p=P, e=2)
         x_first = [sum(X_CHUNKS[:c]) for c in range(len(X_CHUNKS))]
         w_first = [sum(W_CHUNKS[:c]) for c in range(len(W_CHUNKS))]
         x_chunk_of_pass = [c for c in range(len(X_CHUNKS)) for repeat in range(X_CHUNKS[c])]
@@ -65,15 +65,16 @@ def tile_lintrans_pa_k_kernel(tc, x, W1, b1, W2, b2, clusters, out_0, out_1):
 
         def load_w(c):
             first, count = w_first[c], W_CHUNKS[c]
-            w_raw[c] = w_pool.tile([P, max(W_CHUNKS), PACK * H0], BF16, name="w_raw")
+            w_raw[c] = w_pool.tile([P, 2 * max(W_CHUNKS), 2 * H0], BF16, name="w_raw")
             nc.sync.dma_start(
-                out=w_raw[c][:, 0:count, :], in_=w_rows[:, first : first + count, :]
+                out=w_raw[c][:, 0 : 2 * count, :],
+                in_=w_rows[:, 2 * first : 2 * (first + count), :],
             )
 
         loads = []
         for c in range(len(X_CHUNKS)):
             freed = x_first[c - X_BUFS + 1] - 1 if c >= X_BUFS else -1
-            loads.append((x_first[c] - LEAD, freed, "x", c))
+            loads.append((x_first[c] - X_AHEAD, freed, "x", c))
         for c in range(len(W_CHUNKS)):
             freed = w_first[c - W_BUFS + 1] - 1 + LEAD if c >= W_BUFS else -1
             loads.append((w_first[c], freed, "w", c))
@@ -195,23 +196,25 @@ def tile_lintrans_pa_k_kernel(tc, x, W1, b1, W2, b2, clusters, out_0, out_1):
         transposed = {}
         codes = {}
         acc = [acc_pool.tile([P, N_ROWS], F32, name="acc%d" % m) for m in range(H0_TILES)]
+        X_PART, W_PART = slice(0, N_ROWS), slice(N_ROWS, N_ROWS + H0)
+        BOTH = slice(0, N_ROWS + H0)
 
-        def new_grouped(kind, g):
-            grouped[kind, g] = grouped_pool.tile(
-                [P, N_ROWS * PACK], BF16, align_bytes=64, name="grouped_" + kind
+        def new_tiles(step):
+            grouped[step] = grouped_pool.tile(
+                [P, (N_ROWS + H0) * PACK], BF16, align_bytes=64, name="grouped"
             )
+            words = code_pool.tile([P, N_ROWS + H0], U32, align_bytes=64, name="words")
+            scales = code_pool.tile([P, N_ROWS + H0], U8, align_bytes=64, name="scales")
+            codes[step] = (words, scales)
 
-        def new_codes(kind, g):
-            pool = x_code_pool if kind == "x" else w_code_pool
-            words = pool.tile([P, N_ROWS], U32, align_bytes=64, name="words_" + kind)
-            scales = pool.tile([P, N_ROWS], U8, align_bytes=64, name="scales_" + kind)
-            codes[kind, g] = (words, scales)
-
-        def regroup_w(engine_copy, g, cols):
+        def regroup_w(engine_copy, step, cols):
+            g = step - LEAD
             c = w_chunk_of_pass[g]
             local = g - w_first[c]
-            rows = w_raw[c][:, local, :].rearrange("p (t n) -> p t n", t=PACK)
-            words = grouped["w", g][:].rearrange("p (n t) -> p n t", t=PACK)
+            rows = w_raw[c][:, 2 * local : 2 * local + 2, :].rearrange(
+                "p u (e n) -> p (u e) n", e=2
+            )
+            words = grouped[step][:, W_PART.start * PACK :].rearrange("p (n t) -> p n t", t=PACK)
             engine_copy(
                 out=words[:, cols, :].rearrange("p (c i) t -> p c t i", i=4),
                 in_=rows[:, :, cols].rearrange("p t (c i) -> p c t i", i=4),
@@ -226,83 +229,79 @@ def tile_lintrans_pa_k_kernel(tc, x, W1, b1, W2, b2, clusters, out_0, out_1):
                 turned = work_pool.tile([P, 2, 2 * P], F32, tag="work")
                 for u in range(2):
                     for j in range(2):
+                        first_word = WORDS * local + P * u
                         nc.tensor.transpose(
                             turned[:, u, P * j : P * (j + 1)],
-                            x_words[:, 2 * bank + j, WORDS * local + u : WORDS * (local + 1) : 2],
+                            x_words[:, 2 * bank + j, first_word : first_word + P],
                             ident[:],
                         )
                 transposed[g].append(turned)
 
         def copy_x(g):
-            pairs = grouped["x", g][:].bitcast(F32).rearrange("p (c u) -> p c u", u=2)
+            pairs = grouped[g][:].bitcast(F32)[:, 0 : N_ROWS * 2].rearrange(
+                "p (c u) -> p c u", u=2
+            )
             for bank in range(2):
                 nc.scalar.copy(
                     out=pairs[:, 2 * P * bank : 2 * P * (bank + 1), :],
                     in_=transposed[g][bank][:].rearrange("p u c -> p c u"),
                 )
 
-        def quantise(kind, g, cols):
-            words, scales = codes[kind, g]
+        def quantise(step, cols):
+            words, scales = codes[step]
             nc.vector.quantize_mx(
                 out=words[:, cols].bitcast(FP8X4),
                 scales=scales[:, cols],
-                in_=grouped[kind, g][:, PACK * cols.start : PACK * cols.stop],
+                in_=grouped[step][:, PACK * cols.start : PACK * cols.stop],
             )
 
         def multiply(g, m):
-            x_words, x_scales = codes["x", g]
-            w_words, w_scales = codes["w", g]
-            w_cols = slice(P * m, P * (m + 1))
+            x_words, x_scales = codes[g]
+            w_words, w_scales = codes[g + LEAD]
+            w_cols = slice(W_PART.start + P * m, W_PART.start + P * (m + 1))
             nc.tensor.matmul_mx(
                 out=acc[m][:],
                 lhsT=w_words[:, w_cols].bitcast(FP8X4),
                 lhsT_scale=w_scales[:, w_cols],
-                rhs=x_words[:].bitcast(FP8X4),
-                rhs_scale=x_scales[:],
+                rhs=x_words[:, X_PART].bitcast(FP8X4),
+                rhs_scale=x_scales[:, X_PART],
                 start=(g == 0),
                 stop=(g == PASSES - 1),
             )
 
-        ALL = slice(0, N_ROWS)
-
-        last = PASSES - 1
-        for step in range(last + LEAD + 2):
-            if step < PASSES and step % 2 == 0:
+        for step in range(PASSES):
+            new_tiles(step)
+            if step % 2 == 0:
                 transpose_x(step)
                 transpose_x(step + 1)
-            if step < PASSES:
-                new_grouped("x", step)
-                copy_x(step)
-            g = step - LEAD
-            if 0 <= g < last:
-                new_grouped("w", g)
-                cut = W_COLS_VECTOR if step < PASSES else W_COLS_VECTOR_LATE
-                regroup_w(nc.vector.tensor_copy, g, slice(0, cut))
-                regroup_w(nc.scalar.copy, g, slice(cut, H0))
+            copy_x(step)
+            if step >= LEAD:
+                regroup_w(nc.vector.tensor_copy, step, slice(0, W_COLS_VECTOR))
+                regroup_w(nc.scalar.copy, step, slice(W_COLS_VECTOR, H0))
             issue_loads(step)
             if step in small_work:
                 small_work[step]()
-            if 1 <= step <= PASSES:
-                new_codes("x", step - 1)
-                quantise("x", step - 1, ALL)
-            if 0 <= g - 1 < last:
-                new_codes("w", g - 1)
-                quantise("w", g - 1, ALL)
-            if 0 <= g - 2 < last:
+            if step >= 1:
+                quantise(step - 1, BOTH if step - 1 >= LEAD else X_PART)
+            if step >= LEAD + 2:
                 for m in range(H0_TILES):
-                    multiply(g - 2, m)
+                    multiply(step - LEAD - 2, m)
 
         w_tile = [slice(P * m, P * (m + 1)) for m in range(H0_TILES)]
-        new_grouped("w", last)
-        new_codes("w", last)
-        regroup_w(nc.scalar.copy, last, w_tile[3])
-        regroup_w(nc.vector.tensor_copy, last, w_tile[0])
-        regroup_w(nc.vector.tensor_copy, last, w_tile[1])
-        quantise("w", last, w_tile[0])
-        regroup_w(nc.vector.tensor_copy, last, w_tile[2])
-        for m in range(1, H0_TILES):
-            quantise("w", last, w_tile[m])
-        for m in range(H0_TILES):
+        last = PASSES - 1
+        new_tiles(PASSES)
+        quantise(last, BOTH)
+        for g in [last - 2, last - 1]:
+            for m in range(H0_TILES):
+                multiply(g, m)
+        for m in [2, 3]:
+            regroup_w(nc.scalar.copy, PASSES, w_tile[m])
+        for m in [0, 1]:
+            regroup_w(nc.vector.tensor_copy, PASSES, w_tile[m])
+        LAST_ORDER = [0, 2, 1, 3]
+        for m in LAST_ORDER:
+            quantise(PASSES, slice(W_PART.start + P * m, W_PART.start + P * (m + 1)))
+        for m in LAST_ORDER:
             multiply(last, m)
 
         PART_TILES = [[0], [1], [2, 3]]

@@ -23,15 +23,14 @@ WORDS = K_PASS // 2
 
 FLOPS = 2 * N_ROWS * D_IN * H0 + 2 * N_ROWS * H0 * H1 + 3 * N_ROWS * H1 * N_CLUSTERS
 
-X_CHUNKS = [1, 1, 2, 2, 2] + [4] * 5 + [2, 2]
-W_CHUNKS = [1] * 4 + [2] * 12 + [1] * 4
+X_CHUNKS = [4] * 6 + [2] * 3 + [1, 1]
+W_CHUNKS = [4] * 4 + [2] * 7 + [1, 1]
 assert sum(X_CHUNKS) == sum(W_CHUNKS) == PASSES
-X_BUFS, W_BUFS = 4, 8
+X_BUFS, W_BUFS = 4, 4
 LEAD = 1
+X_AHEAD = LEAD + 0.5
 
-X_AHEAD = 1.5
-
-W_COLS_VECTOR = 320
+W_COLS_VECTOR = 336
 
 
 def tile_lintrans_pa_k_kernel(tc, x, W1, b1, W2, b2, clusters, out_0, out_1):
@@ -98,19 +97,19 @@ def tile_lintrans_pa_k_kernel(tc, x, W1, b1, W2, b2, clusters, out_0, out_1):
         B1_ROW, B2_ROW, CLUSTER_ROW, CLUSTER_PITCH = 0, 4, 32, 32
         small_rows = const.tile([P, P], BF16)
         nc.gpsimd.memset(small_rows[:], 0.0)
-        nc.sync.dma_start(
+        nc.gpsimd.dma_start(
             out=small_rows[B1_ROW : B1_ROW + H0_TILES, :], in_=b1.rearrange("(m p) -> m p", p=P)
         )
-        nc.sync.dma_start(
+        nc.gpsimd.dma_start(
             out=small_rows[B2_ROW : B2_ROW + H1_TILES, :], in_=b2.rearrange("(m p) -> m p", p=P)
         )
         for half in range(H1_TILES):
             row = CLUSTER_ROW + CLUSTER_PITCH * half
-            nc.sync.dma_start(
+            nc.gpsimd.dma_start(
                 out=small_rows[row : row + N_CLUSTERS, :], in_=clusters[:, P * half : P * (half + 1)]
             )
         w2_raw = const.tile([P, PACK, H1], BF16)
-        nc.sync.dma_start(out=w2_raw[:], in_=W2.rearrange("(t p) j -> p t j", p=P))
+        nc.gpsimd.dma_start(out=w2_raw[:], in_=W2.rearrange("(t p) j -> p t j", p=P))
         table_warm = const.tile([P, 1], F32)
         nc.scalar.activation(out=table_warm[:], in_=ones[:, 0:1], func=ACT.Silu)
 

@@ -273,10 +273,10 @@ def tile_lintrans_pa_k_kernel(tc, x, W1, b1, W2, b2, clusters, out_0, out_1):
             if step % 2 == 0:
                 transpose_x(step)
                 transpose_x(step + 1)
-            copy_x(step)
             if step >= LEAD:
                 regroup_w(nc.vector.tensor_copy, step, slice(0, W_COLS_VECTOR))
                 regroup_w(nc.scalar.copy, step, slice(W_COLS_VECTOR, H0))
+            copy_x(step)
             issue_loads(step)
             if step in small_work:
                 small_work[step]()
@@ -287,19 +287,20 @@ def tile_lintrans_pa_k_kernel(tc, x, W1, b1, W2, b2, clusters, out_0, out_1):
                     multiply(step - LEAD - 2, m)
 
         w_tile = [slice(P * m, P * (m + 1)) for m in range(H0_TILES)]
+        coded_tile = [slice(W_PART.start + P * m, W_PART.start + P * (m + 1)) for m in range(H0_TILES)]
         last = PASSES - 1
         new_tiles(PASSES)
-        quantise(last, BOTH)
+        quantise(last, W_PART)
+        quantise(last, X_PART)
         for g in [last - 2, last - 1]:
             for m in range(H0_TILES):
                 multiply(g, m)
-        for m in [2, 3]:
+        for m in [1, 2, 3]:
             regroup_w(nc.scalar.copy, PASSES, w_tile[m])
-        for m in [0, 1]:
-            regroup_w(nc.vector.tensor_copy, PASSES, w_tile[m])
-        LAST_ORDER = [0, 2, 1, 3]
+        regroup_w(nc.vector.tensor_copy, PASSES, w_tile[0])
+        LAST_ORDER = [1, 0, 2, 3]
         for m in LAST_ORDER:
-            quantise(PASSES, slice(W_PART.start + P * m, W_PART.start + P * (m + 1)))
+            quantise(PASSES, coded_tile[m])
         for m in LAST_ORDER:
             multiply(last, m)
 
@@ -319,7 +320,7 @@ def tile_lintrans_pa_k_kernel(tc, x, W1, b1, W2, b2, clusters, out_0, out_1):
             )
 
         for a in range(PARTS):
-            for m in range(H0_TILES):
+            for m in LAST_ORDER:
                 silu(m, part_cols[a])
 
         h_grouped = const.tile([P, N_ROWS, PACK], BF16, align_bytes=64)
@@ -415,23 +416,23 @@ def tile_lintrans_pa_k_kernel(tc, x, W1, b1, W2, b2, clusters, out_0, out_1):
                         stop=(m == H1_TILES - 1),
                     )
 
-        def add_b2(a):
+        def add_b2(a, tiles):
+            count = tiles.stop - tiles.start
+            first = tiles.start - PART_TILES[a][0]
             nc.vector.tensor_tensor(
-                out=z_sb[:, part_tiles[a], :],
-                in0=z_psum[a][:],
-                in1=b2_spread[:].unsqueeze(1).to_broadcast([P, len(PART_TILES[a]), H1]),
+                out=z_sb[:, tiles, :],
+                in0=z_psum[a][:, first : first + count, :],
+                in1=b2_spread[:].unsqueeze(1).to_broadcast([P, count, H1]),
                 op=ALU.add,
             )
-            nc.sync.dma_start(out=z_out[:, part_tiles[a], :], in_=z_sb[:, part_tiles[a], :])
 
-        def square_z(a):
-            for i in PART_TILES[a]:
-                nc.scalar.activation(
-                    out=z_squared[:],
-                    in_=z_sb[:, i, :],
-                    func=ACT.Square,
-                    accum_out=z_norm[:, i : i + 1],
-                )
+        def store_z(tiles):
+            nc.sync.dma_start(out=z_out[:, tiles, :], in_=z_sb[:, tiles, :])
+
+        def square_z(i):
+            nc.scalar.activation(
+                out=z_squared[:], in_=z_sb[:, i, :], func=ACT.Square, accum_out=z_norm[:, i : i + 1]
+            )
 
         regroup_h(0)
         quantise_h(0)
@@ -448,15 +449,18 @@ def tile_lintrans_pa_k_kernel(tc, x, W1, b1, W2, b2, clusters, out_0, out_1):
         quantise_h(2)
         second_matmul(2)
         cross_term(1)
-        add_b2(0)
-        add_b2(1)
+        add_b2(0, part_tiles[0])
+        add_b2(1, part_tiles[1])
+        store_z(slice(0, 2))
         square_z(0)
         zt_by_scalar(2, 0)
         zt_by_vector(2, 1)
         cross_term(2)
-        add_b2(2)
         square_z(1)
-        square_z(2)
+        for i in PART_TILES[2]:
+            add_b2(2, slice(i, i + 1))
+            square_z(i)
+        store_z(part_tiles[2])
 
         one_plus_d2 = const.tile(q_shape, F32)
         t_kernel = const.tile(q_shape, F32)

from contextlib import ExitStack

import concourse.mybir as mybir
from concourse.masks import make_identity

F32 = mybir.dt.float32
BF16 = mybir.dt.bfloat16
U32 = mybir.dt.uint32
U8 = mybir.dt.uint8
FP8X4 = mybir.dt.float8_e4m3fn_x4
ACT = mybir.ActivationFunctionType
ALU = mybir.AluOpType

P = 128
PACK = 4
K_PASS = P * PACK
N_ROWS, D_IN, H0, H1, N_CLUSTERS = 512, 16384, 512, 256, 20
ROW_TILES = N_ROWS // P
H0_TILES = H0 // P
H1_TILES = H1 // P
PASSES = D_IN // K_PASS
WORDS = K_PASS // 2

FLOPS = 2 * N_ROWS * D_IN * H0 + 2 * N_ROWS * H0 * H1 + 3 * N_ROWS * H1 * N_CLUSTERS

X_CHUNKS = [4] * 6 + [2] * 3 + [1, 1]
W_CHUNKS = [4] * 4 + [2] * 7 + [1, 1]
assert sum(X_CHUNKS) == sum(W_CHUNKS) == PASSES
X_BUFS, W_BUFS = 4, 4
LEAD = 1
X_AHEAD = LEAD + 0.5

W_COLS_VECTOR = 336


def tile_lintrans_pa_k_kernel(tc, x, W1, b1, W2, b2, clusters, out_0, out_1):
    nc = tc.nc
    with ExitStack() as ctx:
        const = ctx.enter_context(tc.tile_pool(name="const", bufs=1))
        x_pool = ctx.enter_context(tc.tile_pool(name="x_pool", bufs=X_BUFS))
        w_pool = ctx.enter_context(tc.tile_pool(name="w_pool", bufs=W_BUFS))
        grouped_pool = ctx.enter_context(tc.tile_pool(name="grouped_pool", bufs=3))
        code_pool = ctx.enter_context(tc.tile_pool(name="code_pool", bufs=6))
        acc_pool = ctx.enter_context(tc.psum_pool(name="acc_pool", bufs=1))
        work_pool = ctx.enter_context(tc.psum_pool(name="work_pool", bufs=4))
        ctx.enter_context(tc.manual_schedule())

        x_rows = x.rearrange("(p i) k -> p i k", i=ROW_TILES)
        w_rows = W1.rearrange("(s p e) n -> p s (e n)", p=P, e=2)
        x_first = [sum(X_CHUNKS[:c]) for c in range(len(X_CHUNKS))]
        w_first = [sum(W_CHUNKS[:c]) for c in range(len(W_CHUNKS))]
        x_chunk_of_pass = [c for c in range(len(X_CHUNKS)) for repeat in range(X_CHUNKS[c])]
        w_chunk_of_pass = [c for c in range(len(W_CHUNKS)) for repeat in range(W_CHUNKS[c])]
        x_raw = {}
        w_raw = {}

        def load_x(c):
            first, count = x_first[c], X_CHUNKS[c]
            x_raw[c] = x_pool.tile([P, ROW_TILES, max(X_CHUNKS) * K_PASS], BF16, name="x_raw")
            nc.sync.dma_start(
                out=x_raw[c][:, :, 0 : count * K_PASS],
                in_=x_rows[:, :, first * K_PASS : (first + count) * K_PASS],
            )

        def load_w(c):
            first, count = w_first[c], W_CHUNKS[c]
            w_raw[c] = w_pool.tile([P, 2 * max(W_CHUNKS), 2 * H0], BF16, name="w_raw")
            nc.sync.dma_start(
                out=w_raw[c][:, 0 : 2 * count, :],
                in_=w_rows[:, 2 * first : 2 * (first + count), :],
            )

        loads = []
        for c in range(len(X_CHUNKS)):
            freed = x_first[c - X_BUFS + 1] - 1 if c >= X_BUFS else -1
            loads.append((x_first[c] - X_AHEAD, freed, "x", c))
        for c in range(len(W_CHUNKS)):
            freed = w_first[c - W_BUFS + 1] - 1 + LEAD if c >= W_BUFS else -1
            loads.append((w_first[c], freed, "w", c))
        loads = sorted(loads, key=lambda load: load[0])

        def issue_loads(step):
            while loads and loads[0][1] <= step:
                place, freed, kind, c = loads[0]
                loads.remove(loads[0])
                if kind == "x":
                    load_x(c)
                else:
                    load_w(c)

        issue_loads(-1)

        ident = const.tile([P, P], F32)
        make_identity(nc, ident[:])
        ones = const.tile([P, P], F32)
        nc.gpsimd.memset(ones[:], 1.0)
        B1_ROW, B2_ROW, CLUSTER_ROW, CLUSTER_PITCH = 0, 4, 32, 32
        small_rows = const.tile([P, P], BF16)
        nc.gpsimd.memset(small_rows[:], 0.0)
        nc.gpsimd.dma_start(
            out=small_rows[B1_ROW : B1_ROW + H0_TILES, :], in_=b1.rearrange("(m p) -> m p", p=P)
        )
        nc.gpsimd.dma_start(
            out=small_rows[B2_ROW : B2_ROW + H1_TILES, :], in_=b2.rearrange("(m p) -> m p", p=P)
        )
        for half in range(H1_TILES):
            row = CLUSTER_ROW + CLUSTER_PITCH * half
            nc.gpsimd.dma_start(
                out=small_rows[row : row + N_CLUSTERS, :], in_=clusters[:, P * half : P * (half + 1)]
            )
        w2_raw = const.tile([P, PACK, H1], BF16)
        nc.gpsimd.dma_start(out=w2_raw[:], in_=W2.rearrange("(t p) j -> p t j", p=P))
        table_warm = const.tile([P, 1], F32)
        nc.scalar.activation(out=table_warm[:], in_=ones[:, 0:1], func=ACT.Silu)

        small_cols = const.tile([P, P], F32)
        b1_col = small_cols[:, B1_ROW : B1_ROW + H0_TILES]
        b2_col = small_cols[:, B2_ROW : B2_ROW + H1_TILES]
        clusters_t = small_cols[
            :, CLUSTER_ROW : CLUSTER_ROW + CLUSTER_PITCH * H1_TILES
        ].rearrange("p (m k) -> p m k", m=H1_TILES)[:, :, 0:N_CLUSTERS]
        minus_2c = const.tile([P, H1_TILES, N_CLUSTERS], F32)
        c_squared = const.tile([P, H1_TILES, N_CLUSTERS], F32)
        b2_spread = const.tile([P, H1], F32)
        c_norm_plus_1 = const.tile([P, N_CLUSTERS], F32)
        w2_codes = const.tile([P, H1], U32, align_bytes=64)
        w2_scales = const.tile([P, H1], U8, align_bytes=64)

        small_rows_f32 = const.tile([P, P], F32)
        w2_grouped = const.tile([P, H1, PACK], BF16, align_bytes=64)
        small_psum = {}

        def widen_small_rows():
            nc.vector.tensor_copy(out=small_rows_f32[:], in_=small_rows[:])
            nc.vector.tensor_copy(
                out=w2_grouped[:].rearrange("p (c i) t -> p c t i", i=4),
                in_=w2_raw[:].rearrange("p t (c i) -> p c t i", i=4),
            )

        def turn_small_rows_into_columns():
            small_psum["turned"] = work_pool.tile([P, P], F32, tag="work", name="turned")
            nc.tensor.transpose(small_psum["turned"][:], small_rows_f32[:], ident[:])
            nc.vector.quantize_mx(
                out=w2_codes[:].bitcast(FP8X4),
                scales=w2_scales[:],
                in_=w2_grouped[:].rearrange("p j t -> p (j t)"),
            )
            nc.scalar.copy(out=small_cols[:], in_=small_psum["turned"][:])

        def prepare_centroids():
            nc.vector.tensor_scalar(
                out=minus_2c[:], in0=clusters_t, scalar1=-2.0, scalar2=None, op0=ALU.mult
            )
            nc.vector.tensor_tensor(out=c_squared[:], in0=clusters_t, in1=clusters_t, op=ALU.mult)

        def spread_b2_and_centroid_norms():
            spread = work_pool.tile([P, 2 * H1], F32, tag="work", name="spread")
            small_psum["spread"] = spread
            for half in range(H1_TILES):
                nc.tensor.matmul(
                    out=spread[:, P * half : P * (half + 1)],
                    lhsT=b2_col[:, half : half + 1].to_broadcast([P, P]),
                    rhs=ident[:],
                    start=True,
                    stop=True,
                )
            for half in range(H1_TILES):
                nc.tensor.matmul(
                    out=spread[:, H1 : H1 + N_CLUSTERS],
                    lhsT=ones[:],
                    rhs=c_squared[:, half, :],
                    start=(half == 0),
                    stop=(half == H1_TILES - 1),
                )
            nc.scalar.copy(out=b2_spread[:], in_=spread[:, 0:H1])

        def add_1_to_centroid_norms():
            nc.vector.tensor_scalar(
                out=c_norm_plus_1[:],
                in0=small_psum["spread"][:, H1 : H1 + N_CLUSTERS],
                scalar1=1.0,
                scalar2=None,
                op0=ALU.add,
            )

        small_work = {
            PASSES // 2: widen_small_rows,
            PASSES // 2 + 1: turn_small_rows_into_columns,
            PASSES // 2 + 2: prepare_centroids,
            PASSES // 2 + 3: spread_b2_and_centroid_norms,
            PASSES // 2 + 4: add_1_to_centroid_norms,
        }

        grouped = {}
        transposed = {}
        codes = {}
        acc = [acc_pool.tile([P, N_ROWS], F32, name="acc%d" % m) for m in range(H0_TILES)]
        X_PART, W_PART = slice(0, N_ROWS), slice(N_ROWS, N_ROWS + H0)
        BOTH = slice(0, N_ROWS + H0)

        def new_tiles(step):
            grouped[step] = grouped_pool.tile(
                [P, (N_ROWS + H0) * PACK], BF16, align_bytes=64, name="grouped"
            )
            words = code_pool.tile([P, N_ROWS + H0], U32, align_bytes=64, name="words")
            scales = code_pool.tile([P, N_ROWS + H0], U8, align_bytes=64, name="scales")
            codes[step] = (words, scales)

        def regroup_w(engine_copy, step, cols):
            g = step - LEAD
            c = w_chunk_of_pass[g]
            local = g - w_first[c]
            rows = w_raw[c][:, 2 * local : 2 * local + 2, :].rearrange(
                "p u (e n) -> p (u e) n", e=2
            )
            words = grouped[step][:, W_PART.start * PACK :].rearrange("p (n t) -> p n t", t=PACK)
            engine_copy(
                out=words[:, cols, :].rearrange("p (c i) t -> p c t i", i=4),
                in_=rows[:, :, cols].rearrange("p t (c i) -> p c t i", i=4),
            )

        def transpose_x(g):
            c = x_chunk_of_pass[g]
            local = g - x_first[c]
            x_words = x_raw[c][:].bitcast(F32)
            transposed[g] = []
            for bank in range(2):
                turned = work_pool.tile([P, 2, 2 * P], F32, tag="work")
                for u in range(2):
                    for j in range(2):
                        first_word = WORDS * local + P * u
                        nc.tensor.transpose(
                            turned[:, u, P * j : P * (j + 1)],
                            x_words[:, 2 * bank + j, first_word : first_word + P],
                            ident[:],
                        )
                transposed[g].append(turned)

        def copy_x(g):
            pairs = grouped[g][:].bitcast(F32)[:, 0 : N_ROWS * 2].rearrange(
                "p (c u) -> p c u", u=2
            )
            for bank in range(2):
                nc.scalar.copy(
                    out=pairs[:, 2 * P * bank : 2 * P * (bank + 1), :],
                    in_=transposed[g][bank][:].rearrange("p u c -> p c u"),
                )

        def quantise(step, cols):
            words, scales = codes[step]
            nc.vector.quantize_mx(
                out=words[:, cols].bitcast(FP8X4),
                scales=scales[:, cols],
                in_=grouped[step][:, PACK * cols.start : PACK * cols.stop],
            )

        def multiply(g, m):
            x_words, x_scales = codes[g]
            w_words, w_scales = codes[g + LEAD]
            w_cols = slice(W_PART.start + P * m, W_PART.start + P * (m + 1))
            nc.tensor.matmul_mx(
                out=acc[m][:],
                lhsT=w_words[:, w_cols].bitcast(FP8X4),
                lhsT_scale=w_scales[:, w_cols],
                rhs=x_words[:, X_PART].bitcast(FP8X4),
                rhs_scale=x_scales[:, X_PART],
                start=(g == 0),
                stop=(g == PASSES - 1),
            )

        for step in range(PASSES):
            new_tiles(step)
            if step % 2 == 0:
                transpose_x(step)
                transpose_x(step + 1)
            if step >= LEAD:
                regroup_w(nc.vector.tensor_copy, step, slice(0, W_COLS_VECTOR))
                regroup_w(nc.scalar.copy, step, slice(W_COLS_VECTOR, H0))
            copy_x(step)
            issue_loads(step)
            if step in small_work:
                small_work[step]()
            if step >= 1:
                quantise(step - 1, BOTH if step - 1 >= LEAD else X_PART)
            if step >= LEAD + 2:
                for m in range(H0_TILES):
                    multiply(step - LEAD - 2, m)

        w_tile = [slice(P * m, P * (m + 1)) for m in range(H0_TILES)]
        coded_tile = [slice(W_PART.start + P * m, W_PART.start + P * (m + 1)) for m in range(H0_TILES)]
        last = PASSES - 1
        new_tiles(PASSES)
        quantise(last, W_PART)
        quantise(last, X_PART)
        for g in [last - 2, last - 1]:
            for m in range(H0_TILES):
                multiply(g, m)
        for m in [1, 2, 3]:
            regroup_w(nc.scalar.copy, PASSES, w_tile[m])
        regroup_w(nc.vector.tensor_copy, PASSES, w_tile[0])
        LAST_ORDER = [1, 0, 2, 3]
        for m in LAST_ORDER:
            quantise(PASSES, coded_tile[m])
        for m in LAST_ORDER:
            multiply(last, m)

        PART_TILES = [[0], [1], [2, 3]]
        PARTS = len(PART_TILES)
        part_cols = [slice(P * t[0], P * (t[-1] + 1)) for t in PART_TILES]
        part_tiles = [slice(t[0], t[-1] + 1) for t in PART_TILES]

        h_planes = const.tile([P, PACK, N_ROWS], BF16)

        def silu(m, cols):
            nc.scalar.activation(
                out=h_planes[:, m, cols],
                in_=acc[m][:, cols],
                func=ACT.Silu,
                bias=b1_col[:, m : m + 1],
            )

        for a in range(PARTS):
            for m in LAST_ORDER:
                silu(m, part_cols[a])

        h_grouped = const.tile([P, N_ROWS, PACK], BF16, align_bytes=64)
        h_codes = const.tile([P, N_ROWS], U32, align_bytes=64)
        h_scales = const.tile([P, N_ROWS], U8, align_bytes=64)

        def regroup_h(a):
            nc.vector.tensor_copy(
                out=h_grouped[:, part_cols[a], :].rearrange("p (c i) t -> p c t i", i=4),
                in_=h_planes[:, :, part_cols[a]].rearrange("p t (c i) -> p c t i", i=4),
            )

        def quantise_h(a):
            nc.vector.quantize_mx(
                out=h_codes[:, part_cols[a]].bitcast(FP8X4),
                scales=h_scales[:, part_cols[a]],
                in_=h_grouped[:, part_cols[a], :].rearrange("p c t -> p (c t)"),
            )

        zt_psum = {}
        z_psum = {}
        Z_BANK = ["acc0", "acc2", "acc3"]

        def second_matmul(a):
            for m in range(H1_TILES):
                zt_psum[a, m] = work_pool.tile(
                    [P, P * len(PART_TILES[a])], F32, tag="work", name="zt_psum"
                )
                j_cols = slice(P * m, P * (m + 1))
                nc.tensor.matmul_mx(
                    out=zt_psum[a, m][:],
                    lhsT=w2_codes[:, j_cols].bitcast(FP8X4),
                    lhsT_scale=w2_scales[:, j_cols],
                    rhs=h_codes[:, part_cols[a]].bitcast(FP8X4),
                    rhs_scale=h_scales[:, part_cols[a]],
                    start=True,
                    stop=True,
                )
            z_psum[a] = acc_pool.tile(
                [P, len(PART_TILES[a]), H1], F32, tag=Z_BANK[a], name="z_psum"
            )
            for i in PART_TILES[a]:
                row_cols = slice(P * i, P * (i + 1))
                nc.tensor.matmul_mx(
                    out=z_psum[a][:, i - PART_TILES[a][0], :],
                    lhsT=h_codes[:, row_cols].bitcast(FP8X4),
                    lhsT_scale=h_scales[:, row_cols],
                    rhs=w2_codes[:].bitcast(FP8X4),
                    rhs_scale=w2_scales[:],
                    start=True,
                    stop=True,
                )

        CLUSTER_SLOT = 32
        q_shape = [P, ROW_TILES, N_CLUSTERS]
        zt = const.tile([P, H1_TILES, N_ROWS], F32)
        z_sb = const.tile([P, ROW_TILES, H1], F32)
        z_squared = const.tile([P, H1], F32)
        z_norm = const.tile([P, ROW_TILES], F32)
        norms = const.tile(q_shape, F32)
        cross = {}
        z_out = out_0.rearrange("(p i) j -> p i j", i=ROW_TILES)

        def zt_by_scalar(a, m):
            nc.scalar.activation(
                out=zt[:, m, part_cols[a]],
                in_=zt_psum[a, m][:],
                func=ACT.Identity,
                bias=b2_col[:, m : m + 1],
            )

        def zt_by_vector(a, m):
            nc.vector.tensor_scalar(
                out=zt[:, m, part_cols[a]],
                in0=zt_psum[a, m][:],
                scalar1=b2_col[:, m : m + 1],
                scalar2=None,
                op0=ALU.add,
            )

        def cross_term(a):
            if a == 0:
                cross[0] = acc_pool.tile([P, 2, CLUSTER_SLOT], F32, tag="acc1", name="cross_early")
            if a == 2:
                cross[1] = work_pool.tile([P, 2, CLUSTER_SLOT], F32, tag="work", name="cross_late")
            for i in PART_TILES[a]:
                for m in range(H1_TILES):
                    nc.tensor.matmul(
                        out=cross[i // 2][:, i % 2, 0:N_CLUSTERS],
                        lhsT=zt[:, m, P * i : P * (i + 1)],
                        rhs=minus_2c[:, m, :],
                        start=(m == 0),
                        stop=(m == H1_TILES - 1),
                    )

        def add_b2(a, tiles):
            count = tiles.stop - tiles.start
            first = tiles.start - PART_TILES[a][0]
            nc.vector.tensor_tensor(
                out=z_sb[:, tiles, :],
                in0=z_psum[a][:, first : first + count, :],
                in1=b2_spread[:].unsqueeze(1).to_broadcast([P, count, H1]),
                op=ALU.add,
            )

        def store_z(tiles):
            nc.sync.dma_start(out=z_out[:, tiles, :], in_=z_sb[:, tiles, :])

        def square_z(i):
            nc.scalar.activation(
                out=z_squared[:], in_=z_sb[:, i, :], func=ACT.Square, accum_out=z_norm[:, i : i + 1]
            )

        regroup_h(0)
        quantise_h(0)
        second_matmul(0)
        regroup_h(1)
        quantise_h(1)
        second_matmul(1)
        zt_by_scalar(0, 0)
        zt_by_vector(0, 1)
        cross_term(0)
        regroup_h(2)
        zt_by_scalar(1, 0)
        zt_by_vector(1, 1)
        quantise_h(2)
        second_matmul(2)
        cross_term(1)
        add_b2(0, part_tiles[0])
        add_b2(1, part_tiles[1])
        store_z(slice(0, 2))
        square_z(0)
        zt_by_scalar(2, 0)
        zt_by_vector(2, 1)
        cross_term(2)
        square_z(1)
        for i in PART_TILES[2]:
            add_b2(2, slice(i, i + 1))
            square_z(i)
        store_z(part_tiles[2])

        one_plus_d2 = const.tile(q_shape, F32)
        t_kernel = const.tile(q_shape, F32)
        t_sum = const.tile([P, ROW_TILES], F32)
        t_sum_inverse = const.tile([P, ROW_TILES], F32)
        q_sb = const.tile(q_shape, F32)

        def add_norms(tiles, shape):
            nc.vector.tensor_tensor(
                out=norms[:, tiles, :],
                in0=c_norm_plus_1[:].unsqueeze(1).to_broadcast(shape),
                in1=z_norm[:, tiles].unsqueeze(2).to_broadcast(shape),
                op=ALU.add,
            )

        def kernel_of_distances(tiles):
            nc.vector.tensor_tensor(
                out=one_plus_d2[:, tiles, :],
                in0=cross[tiles.start // 2][:, :, 0:N_CLUSTERS],
                in1=norms[:, tiles, :],
                op=ALU.add,
            )
            nc.vector.reciprocal(out=t_kernel[:, tiles, :], in_=one_plus_d2[:, tiles, :])
            nc.vector.tensor_reduce(
                out=t_sum[:, tiles], in_=t_kernel[:, tiles, :], axis=mybir.AxisListType.X, op=ALU.add
            )

        early, late = slice(0, 2), slice(2, ROW_TILES)
        pair_shape = [P, 2, N_CLUSTERS]
        for tiles in [early, late]:
            add_norms(tiles, pair_shape)
            kernel_of_distances(tiles)
        nc.vector.reciprocal(out=t_sum_inverse[:], in_=t_sum[:])
        nc.vector.tensor_tensor(
            out=q_sb[:],
            in0=t_kernel[:],
            in1=t_sum_inverse[:].unsqueeze(2).to_broadcast(q_shape),
            op=ALU.mult,
        )
        nc.sync.dma_start(out=out_1.rearrange("(p i) k -> p i k", i=ROW_TILES), in_=q_sb[:])
